import numpy as np
import ml_dtypes


def mxq(x, axis, fmt="e4m3"):
    dtype, down = {"e4m3": (ml_dtypes.float8_e4m3fn, 7), "e5m2": (ml_dtypes.float8_e5m2, 14)}[fmt]
    v = np.moveaxis(np.asarray(x, np.float32).astype(ml_dtypes.bfloat16).astype(np.float64), axis, -1)
    blocks = v.reshape(v.shape[:-1] + (-1, 32))
    amax = np.abs(blocks).max(-1, keepdims=True)
    byte = np.maximum(np.where(amax > 0, np.frexp(amax)[1] - 1 + 127, 0) - down, 1)
    scale = np.exp2(byte - 127.0)
    codes = (blocks / scale).astype(np.float32).astype(dtype).astype(np.float64)
    return np.moveaxis((codes * scale).reshape(v.shape), -1, axis)


WIDE = False


def mx_kscale(k):
    if not WIDE:
        return np.ones(k)
    levels = np.array([10, -10, 5, -5, 0])
    a = np.random.permutation(np.resize(levels, k // 512 * 4)).reshape(k // 512, 4)
    idx = np.arange(k)
    return np.exp2(a[idx // 512, idx % 128 // 32])


BF16 = ml_dtypes.bfloat16


def bf(x):
    return np.asarray(x, np.float32).astype(BF16)


def f64(x):
    return np.asarray(x).astype(np.float64)


B, H0, H1, H2 = 1024, 1024, 512, 128
NEG_SLOPE = 0.01
LV_MIN, LV_MAX = -10.0, 10.0


def leaky_relu(v):
    return np.where(v > 0, v, NEG_SLOPE * v)


def setup_inputs():
    s = mx_kscale(H0)
    t = mx_kscale(H1)
    return {"x": bf(np.random.standard_normal((B, H0)) * s),
            "noise_enc": bf(np.random.standard_normal((B, H2))),
            "noise_z": bf(np.random.standard_normal((B, H2))),
            "w1_mu": bf(np.random.standard_normal((H0, H1)) / np.sqrt(H0) / s[:, None] * t),
            "b1_mu": bf(np.random.standard_normal(H1) * 0.5 * t),
            "w2_mu": bf(np.random.standard_normal((H1, H2)) * 6.0 / np.sqrt(H1) / t[:, None]),
            "b2_mu": bf(np.random.standard_normal(H2) * 1.0),
            "w1_sig": bf(np.random.standard_normal((H0, H1)) / np.sqrt(H0) / s[:, None]),
            "b1_sig": bf(np.random.standard_normal(H1) * 0.3),
            "w2_sig": bf(np.random.standard_normal((H1, H2)) * 4.5 / np.sqrt(H1)),
            "b2_sig": bf(np.random.standard_normal(H2) * 0.8)}


def reference(x, noise_enc, noise_z, w1_mu, b1_mu, w2_mu, b2_mu, w1_sig, b1_sig, w2_sig, b2_sig):
    xq = mxq(f64(x), 1, "e4m3")
    h_mu = leaky_relu((xq @ mxq(f64(w1_mu), 0, "e4m3")) + f64(b1_mu))
    mean = leaky_relu((mxq(h_mu, 1, "e4m3") @ mxq(f64(w2_mu), 0, "e4m3")) + f64(b2_mu))
    h_sig = np.tanh((xq @ mxq(f64(w1_sig), 0, "e4m3")) + f64(b1_sig))
    log_var = leaky_relu((mxq(h_sig, 1, "e4m3") @ mxq(f64(w2_sig), 0, "e4m3")) + f64(b2_sig))
    log_var = np.clip(log_var, LV_MIN, LV_MAX)
    std = np.exp(0.5 * log_var)
    z_enc = mean + std * f64(noise_enc)
    z = mean + std * f64(noise_z)
    return z_enc, z

@@ -1,0 +1,261 @@
+from contextlib import ExitStack
+
+import concourse.mybir as mybir
+from concourse.masks import make_identity
+
+F32 = mybir.dt.float32
+BF16 = mybir.dt.bfloat16
+U32 = mybir.dt.uint32
+U8 = mybir.dt.uint8
+FP8X4 = mybir.dt.float8_e4m3fn_x4
+ALU = mybir.AluOpType
+ACT = mybir.ActivationFunctionType
+
+P = 128
+PACK = 4
+K_PASS = P * PACK
+
+B, H0, H1, H2 = 1024, 1024, 512, 128
+NEG_SLOPE = 0.01
+LV_MIN, LV_MAX = -10.0, 10.0
+
+B_TILES = B // P
+PAIRS = B_TILES // 2
+PAIR_COLS = 2 * P
+PASSES1 = H0 // K_PASS
+H_TILES = H1 // P
+CHUNKS = 2
+CHUNK_TILES = B_TILES // CHUNKS
+CHUNK_COLS = CHUNK_TILES * P
+
+MU, SIG = 0, 1
+
+FLOPS = 2 * (2 * B * H0 * H1 + 2 * B * H1 * H2)
+
+
+def interleave_rows(copy, grouped, planes):
+    copy(
+        out=grouped.rearrange("p (c i) t -> p c t i", i=4),
+        in_=planes.rearrange("p t (c i) -> p c t i", i=4),
+    )
+
+
+def tile_infovae_pa_kernel(
+    tc, x, noise_enc, noise_z, w1_mu, b1_mu, w2_mu, b2_mu, w1_sig, b1_sig, w2_sig, b2_sig, out_0, out_1
+):
+    nc = tc.nc
+    w1 = (w1_mu, w1_sig)
+    w2 = (w2_mu, w2_sig)
+    b1 = (b1_mu, b1_sig)
+    b2 = (b2_mu, b2_sig)
+
+    with ExitStack() as ctx:
+        keep = ctx.enter_context(tc.tile_pool(name="keep", bufs=1))
+        stage = ctx.enter_context(tc.tile_pool(name="stage", bufs=2))
+        psum_t = ctx.enter_context(tc.psum_pool(name="psum_t", bufs=2))
+        psum_h = ctx.enter_context(tc.psum_pool(name="psum_h", bufs=4))
+        psum_o = ctx.enter_context(tc.psum_pool(name="psum_o", bufs=1))
+
+        b1_rows = keep.tile([P, P], BF16)
+        b2_rows = keep.tile([P, 2 * H2], BF16)
+        nc.vector.memset(b1_rows[:], 0.0)
+        nc.vector.memset(b2_rows[:], 0.0)
+        for r in (MU, SIG):
+            nc.scalar.dma_start(
+                out=b1_rows[H_TILES * r : H_TILES * (r + 1), :], in_=b1[r].rearrange("(m p) -> m p", p=P)
+            )
+            nc.scalar.dma_start(
+                out=b2_rows[0:1, H2 * r : H2 * (r + 1)], in_=b2[r].rearrange("(a o) -> a o", a=1)
+            )
+
+        x_sb = keep.tile([P, B_TILES, H0], BF16)
+        x_rows = x.rearrange("(p i) k -> p i k", i=B_TILES)
+        w1_raw = keep.tile([P, 2, PASSES1, PACK, H1], BF16)
+
+        def load_x_pair(j):
+            nc.sync.dma_start(out=x_sb[:, 2 * j : 2 * j + 2, :], in_=x_rows[:, 2 * j : 2 * j + 2, :])
+
+        def load_w1(r, g):
+            nc.sync.dma_start(
+                out=w1_raw[:, r, g].rearrange("p (u e) c -> p u (e c)", e=2),
+                in_=w1[r][K_PASS * g : K_PASS * (g + 1), :].rearrange("(u p e) c -> p u (e c)", u=2, e=2),
+            )
+
+        load_x_pair(0)
+        load_w1(SIG, 0)
+        load_x_pair(1)
+        load_w1(SIG, 1)
+        load_w1(MU, 0)
+        load_w1(MU, 1)
+        load_x_pair(2)
+        load_x_pair(3)
+
+        ident = keep.tile([P, P], F32)
+        make_identity(nc, ident[:])
+        w2_raw = keep.tile([P, 2, PACK, H2], BF16)
+        noise = keep.tile([P, 2, B_TILES * H2], BF16)
+        for r in (MU, SIG):
+            nc.gpsimd.dma_start(out=w2_raw[:, r], in_=w2[r].rearrange("(m p) o -> p m o", p=P))
+        nc.gpsimd.dma_start(out=noise[:, 0, :], in_=noise_enc.rearrange("(p i) o -> p (i o)", i=B_TILES))
+        nc.gpsimd.dma_start(out=noise[:, 1, :], in_=noise_z.rearrange("(p i) o -> p (i o)", i=B_TILES))
+
+        b1_rows_f32 = keep.tile([P, P], F32)
+        nc.vector.tensor_copy(out=b1_rows_f32[:], in_=b1_rows[:])
+        b1_ps = psum_t.tile([P, P], F32, tag="xt")
+        nc.tensor.transpose(b1_ps[:], b1_rows_f32[:], ident[:])
+        b1_col = keep.tile([P, 2 * H_TILES], F32)
+        nc.vector.tensor_copy(out=b1_col[:], in_=b1_ps[:, 0 : 2 * H_TILES])
+        ones = keep.tile([P, P], BF16)
+        nc.vector.memset(ones[:], 1.0)
+        b2_ps = psum_t.tile([P, 2 * H2], F32, tag="xt")
+        nc.tensor.matmul(b2_ps[:], lhsT=ones[:], rhs=b2_rows[:], start=True, stop=True)
+        b2_all = keep.tile([P, 2 * H2], F32)
+        nc.vector.tensor_copy(out=b2_all[:], in_=b2_ps[:])
+
+        x_codes = keep.tile([P, PASSES1, B], U32, align_bytes=64)
+        x_scales = keep.tile([P, PASSES1, B], U8, align_bytes=64)
+        w1_codes = keep.tile([P, 2, PASSES1, H1], U32, align_bytes=64)
+        w1_scales = keep.tile([P, 2, PASSES1, H1], U8, align_bytes=64)
+
+        def quantise_x_pair(j):
+            cols = slice(PAIR_COLS * j, PAIR_COLS * (j + 1))
+            for g in range(PASSES1):
+                xt = psum_t.tile([P, 2, PAIR_COLS], F32, tag="xt")
+                for ii in range(2):
+                    words = x_sb[:, 2 * j + ii, :].bitcast(F32)
+                    for u in range(2):
+                        first = (K_PASS * g + 2 * P * u) // 2
+                        nc.tensor.transpose(
+                            xt[:, u, P * ii : P * (ii + 1)], words[:, first : first + P], ident[:]
+                        )
+                x_grouped = stage.tile([P, PAIR_COLS * PACK], BF16, align_bytes=64, tag="x_grouped")
+                nc.scalar.copy(
+                    out=x_grouped[:].bitcast(F32).rearrange("p (b u) -> p b u", u=2),
+                    in_=xt[:].rearrange("p u b -> p b u"),
+                )
+                nc.vector.quantize_mx(
+                    out=x_codes[:, g, cols].bitcast(FP8X4), scales=x_scales[:, g, cols], in_=x_grouped[:]
+                )
+
+        def quantise_w1(r, g, copy):
+            w1_grouped = stage.tile([P, H1, PACK], BF16, align_bytes=64, tag="w1_grouped")
+            interleave_rows(copy, w1_grouped[:], w1_raw[:, r, g])
+            nc.vector.quantize_mx(
+                out=w1_codes[:, r, g, :].bitcast(FP8X4),
+                scales=w1_scales[:, r, g, :],
+                in_=w1_grouped[:].rearrange("p c t -> p (c t)"),
+            )
+
+        quantise_x_pair(0)
+        quantise_w1(SIG, 0, nc.vector.tensor_copy)
+        quantise_x_pair(1)
+        quantise_w1(SIG, 1, nc.vector.tensor_copy)
+        quantise_w1(MU, 0, nc.scalar.copy)
+        quantise_w1(MU, 1, nc.scalar.copy)
+        quantise_x_pair(2)
+        quantise_x_pair(3)
+
+        w2_grouped = keep.tile([P, 2, H2, PACK], BF16, align_bytes=64)
+        nc.vector.tensor_copy(out=w2_grouped[:], in_=w2_raw[:].rearrange("p r m o -> p r o m"))
+        w2_codes = keep.tile([P, 2 * H2], U32, align_bytes=64)
+        w2_scales = keep.tile([P, 2 * H2], U8, align_bytes=64)
+        nc.vector.quantize_mx(
+            out=w2_codes[:].bitcast(FP8X4),
+            scales=w2_scales[:],
+            in_=w2_grouped[:].rearrange("p r o m -> p (r o m)"),
+        )
+
+        out_rows = (
+            out_0.rearrange("(p i) o -> p (i o)", i=B_TILES),
+            out_1.rearrange("(p i) o -> p (i o)", i=B_TILES),
+        )
+
+        def hidden_layer(c, r):
+            cols = slice(CHUNK_COLS * c, CHUNK_COLS * (c + 1))
+            planes = stage.tile([P, H_TILES, CHUNK_COLS], BF16 if r == SIG else F32, tag="planes%d" % r)
+            for m in range(H_TILES):
+                units = slice(P * m, P * (m + 1))
+                acc = psum_h.tile([P, CHUNK_COLS], F32, tag="acc")
+                for g in range(PASSES1):
+                    nc.tensor.matmul_mx(
+                        out=acc[:],
+                        lhsT=w1_codes[:, r, g, units].bitcast(FP8X4),
+                        lhsT_scale=w1_scales[:, r, g, units],
+                        rhs=x_codes[:, g, cols].bitcast(FP8X4),
+                        rhs_scale=x_scales[:, g, cols],
+                        start=(g == 0),
+                        stop=(g == PASSES1 - 1),
+                    )
+                nc.scalar.activation(
+                    out=planes[:, m, :],
+                    in_=acc[:],
+                    func=ACT.Tanh if r == SIG else ACT.Identity,
+                    bias=b1_col[:, H_TILES * r + m : H_TILES * r + m + 1],
+                    scale=1.0,
+                )
+            h_grouped = stage.tile([P, CHUNK_COLS, PACK], BF16, align_bytes=64, tag="h_grouped%d" % r)
+            if r == SIG:
+                interleave_rows(nc.scalar.copy, h_grouped[:], planes[:])
+            else:
+                by_column = planes[:].rearrange("p m b -> p b m")
+                nc.vector.scalar_tensor_tensor(
+                    out=h_grouped[:], in0=by_column, scalar=NEG_SLOPE, in1=by_column, op0=ALU.mult, op1=ALU.max
+                )
+            h_codes = stage.tile([P, CHUNK_COLS], U32, align_bytes=64, tag="h_codes%d" % r)
+            h_scales = stage.tile([P, CHUNK_COLS], U8, align_bytes=64, tag="h_scales%d" % r)
+            nc.vector.quantize_mx(
+                out=h_codes[:].bitcast(FP8X4), scales=h_scales[:], in_=h_grouped[:].rearrange("p b m -> p (b m)")
+            )
+            return h_codes, h_scales
+
+        def output_layer(r, h_codes, h_scales):
+            outs = slice(H2 * r, H2 * (r + 1))
+            acc = psum_o.tile([P, CHUNK_TILES, H2], F32, tag="out%d" % r)
+            for i in range(CHUNK_TILES):
+                rows = slice(P * i, P * (i + 1))
+                nc.tensor.matmul_mx(
+                    out=acc[:, i, :],
+                    lhsT=h_codes[:, rows].bitcast(FP8X4),
+                    lhsT_scale=h_scales[:, rows],
+                    rhs=w2_codes[:, outs].bitcast(FP8X4),
+                    rhs_scale=w2_scales[:, outs],
+                    start=True,
+                    stop=True,
+                )
+            biased = stage.tile([P, CHUNK_TILES, H2], F32, tag="biased%d" % r)
+            nc.vector.tensor_tensor(
+                out=biased[:],
+                in0=acc[:],
+                in1=b2_all[:, outs].unsqueeze(1).to_broadcast([P, CHUNK_TILES, H2]),
+                op=ALU.add,
+            )
+            flat = biased[:].rearrange("p i o -> p (i o)")
+            result = stage.tile([P, CHUNK_COLS], F32, tag="lrelu%d" % r)
+            nc.vector.scalar_tensor_tensor(
+                out=result[:], in0=flat, scalar=NEG_SLOPE, in1=flat, op0=ALU.mult, op1=ALU.max
+            )
+            return result
+
+        for c in range(CHUNKS):
+            cols = slice(CHUNK_COLS * c, CHUNK_COLS * (c + 1))
+            sig_codes, sig_scales = hidden_layer(c, SIG)
+            mu_codes, mu_scales = hidden_layer(c, MU)
+
+            log_var = output_layer(SIG, sig_codes, sig_scales)
+            nc.vector.tensor_scalar(
+                out=log_var[:], in0=log_var[:], scalar1=LV_MAX, scalar2=LV_MIN, op0=ALU.min, op1=ALU.max
+            )
+            std = stage.tile([P, CHUNK_COLS], F32, tag="std")
+            nc.scalar.activation(out=std[:], in_=log_var[:], func=ACT.Exp, scale=0.5)
+            mean = output_layer(MU, mu_codes, mu_scales)
+
+            both = [P, 2, CHUNK_COLS]
+            z = stage.tile(both, F32, tag="z")
+            nc.vector.tensor_tensor(
+                out=z[:], in0=noise[:, :, cols], in1=std[:].unsqueeze(1).to_broadcast(both), op=ALU.mult
+            )
+            nc.vector.tensor_tensor(
+                out=z[:], in0=z[:], in1=mean[:].unsqueeze(1).to_broadcast(both), op=ALU.add
+            )
+            for n in range(2):
+                nc.sync.dma_start(out=out_rows[n][:, cols], in_=z[:, n, :])

@@ -24,9 +24,10 @@ PAIRS = B_TILES // 2
 PAIR_COLS = 2 * P
 PASSES1 = H0 // K_PASS
 H_TILES = H1 // P
-CHUNKS = 2
+CHUNKS = PAIRS
 CHUNK_TILES = B_TILES // CHUNKS
 CHUNK_COLS = CHUNK_TILES * P
+W1_VECTOR_COLS = 320
 
 MU, SIG = 0, 1
 
@@ -51,26 +52,33 @@ def tile_infovae_pa_kernel(
 
     with ExitStack() as ctx:
         keep = ctx.enter_context(tc.tile_pool(name="keep", bufs=1))
-        stage = ctx.enter_context(tc.tile_pool(name="stage", bufs=2))
+        stage = ctx.enter_context(tc.tile_pool(name="stage", bufs=3))
         psum_t = ctx.enter_context(tc.psum_pool(name="psum_t", bufs=2))
         psum_h = ctx.enter_context(tc.psum_pool(name="psum_h", bufs=4))
         psum_o = ctx.enter_context(tc.psum_pool(name="psum_o", bufs=1))
 
+        ident = keep.tile([P, P], F32)
+        make_identity(nc, ident[:])
+
         b1_rows = keep.tile([P, P], BF16)
         b2_rows = keep.tile([P, 2 * H2], BF16)
+        ones = keep.tile([P, P], BF16)
         nc.vector.memset(b1_rows[:], 0.0)
         nc.vector.memset(b2_rows[:], 0.0)
+        nc.vector.memset(ones[:], 1.0)
         for r in (MU, SIG):
-            nc.scalar.dma_start(
+            nc.sync.dma_start(
                 out=b1_rows[H_TILES * r : H_TILES * (r + 1), :], in_=b1[r].rearrange("(m p) -> m p", p=P)
             )
-            nc.scalar.dma_start(
+            nc.sync.dma_start(
                 out=b2_rows[0:1, H2 * r : H2 * (r + 1)], in_=b2[r].rearrange("(a o) -> a o", a=1)
             )
 
         x_sb = keep.tile([P, B_TILES, H0], BF16)
         x_rows = x.rearrange("(p i) k -> p i k", i=B_TILES)
         w1_raw = keep.tile([P, 2, PASSES1, PACK, H1], BF16)
+        w2_raw = keep.tile([P, 2, PACK, H2], BF16)
+        noise = keep.tile([P, 2, B_TILES * H2], BF16)
 
         def load_x_pair(j):
             nc.sync.dma_start(out=x_sb[:, 2 * j : 2 * j + 2, :], in_=x_rows[:, 2 * j : 2 * j + 2, :])
@@ -81,23 +89,17 @@ def tile_infovae_pa_kernel(
                 in_=w1[r][K_PASS * g : K_PASS * (g + 1), :].rearrange("(u p e) c -> p u (e c)", u=2, e=2),
             )
 
-        load_x_pair(0)
+        for r in (MU, SIG):
+            nc.sync.dma_start(out=w2_raw[:, r], in_=w2[r].rearrange("(m p) o -> p m o", p=P))
         load_w1(SIG, 0)
-        load_x_pair(1)
+        load_x_pair(0)
         load_w1(SIG, 1)
         load_w1(MU, 0)
         load_w1(MU, 1)
-        load_x_pair(2)
-        load_x_pair(3)
-
-        ident = keep.tile([P, P], F32)
-        make_identity(nc, ident[:])
-        w2_raw = keep.tile([P, 2, PACK, H2], BF16)
-        noise = keep.tile([P, 2, B_TILES * H2], BF16)
-        for r in (MU, SIG):
-            nc.gpsimd.dma_start(out=w2_raw[:, r], in_=w2[r].rearrange("(m p) o -> p m o", p=P))
-        nc.gpsimd.dma_start(out=noise[:, 0, :], in_=noise_enc.rearrange("(p i) o -> p (i o)", i=B_TILES))
-        nc.gpsimd.dma_start(out=noise[:, 1, :], in_=noise_z.rearrange("(p i) o -> p (i o)", i=B_TILES))
+        for j in range(1, PAIRS):
+            load_x_pair(j)
+        nc.sync.dma_start(out=noise[:, 0, :], in_=noise_enc.rearrange("(p i) o -> p (i o)", i=B_TILES))
+        nc.sync.dma_start(out=noise[:, 1, :], in_=noise_z.rearrange("(p i) o -> p (i o)", i=B_TILES))
 
         b1_rows_f32 = keep.tile([P, P], F32)
         nc.vector.tensor_copy(out=b1_rows_f32[:], in_=b1_rows[:])
@@ -105,55 +107,10 @@ def tile_infovae_pa_kernel(
         nc.tensor.transpose(b1_ps[:], b1_rows_f32[:], ident[:])
         b1_col = keep.tile([P, 2 * H_TILES], F32)
         nc.vector.tensor_copy(out=b1_col[:], in_=b1_ps[:, 0 : 2 * H_TILES])
-        ones = keep.tile([P, P], BF16)
-        nc.vector.memset(ones[:], 1.0)
         b2_ps = psum_t.tile([P, 2 * H2], F32, tag="xt")
         nc.tensor.matmul(b2_ps[:], lhsT=ones[:], rhs=b2_rows[:], start=True, stop=True)
         b2_all = keep.tile([P, 2 * H2], F32)
         nc.vector.tensor_copy(out=b2_all[:], in_=b2_ps[:])
-
-        x_codes = keep.tile([P, PASSES1, B], U32, align_bytes=64)
-        x_scales = keep.tile([P, PASSES1, B], U8, align_bytes=64)
-        w1_codes = keep.tile([P, 2, PASSES1, H1], U32, align_bytes=64)
-        w1_scales = keep.tile([P, 2, PASSES1, H1], U8, align_bytes=64)
-
-        def quantise_x_pair(j):
-            cols = slice(PAIR_COLS * j, PAIR_COLS * (j + 1))
-            for g in range(PASSES1):
-                xt = psum_t.tile([P, 2, PAIR_COLS], F32, tag="xt")
-                for ii in range(2):
-                    words = x_sb[:, 2 * j + ii, :].bitcast(F32)
-                    for u in range(2):
-                        first = (K_PASS * g + 2 * P * u) // 2
-                        nc.tensor.transpose(
-                            xt[:, u, P * ii : P * (ii + 1)], words[:, first : first + P], ident[:]
-                        )
-                x_grouped = stage.tile([P, PAIR_COLS * PACK], BF16, align_bytes=64, tag="x_grouped")
-                nc.scalar.copy(
-                    out=x_grouped[:].bitcast(F32).rearrange("p (b u) -> p b u", u=2),
-                    in_=xt[:].rearrange("p u b -> p b u"),
-                )
-                nc.vector.quantize_mx(
-                    out=x_codes[:, g, cols].bitcast(FP8X4), scales=x_scales[:, g, cols], in_=x_grouped[:]
-                )
-
-        def quantise_w1(r, g, copy):
-            w1_grouped = stage.tile([P, H1, PACK], BF16, align_bytes=64, tag="w1_grouped")
-            interleave_rows(copy, w1_grouped[:], w1_raw[:, r, g])
-            nc.vector.quantize_mx(
-                out=w1_codes[:, r, g, :].bitcast(FP8X4),
-                scales=w1_scales[:, r, g, :],
-                in_=w1_grouped[:].rearrange("p c t -> p (c t)"),
-            )
-
-        quantise_x_pair(0)
-        quantise_w1(SIG, 0, nc.vector.tensor_copy)
-        quantise_x_pair(1)
-        quantise_w1(SIG, 1, nc.vector.tensor_copy)
-        quantise_w1(MU, 0, nc.scalar.copy)
-        quantise_w1(MU, 1, nc.scalar.copy)
-        quantise_x_pair(2)
-        quantise_x_pair(3)
 
         w2_grouped = keep.tile([P, 2, H2, PACK], BF16, align_bytes=64)
         nc.vector.tensor_copy(out=w2_grouped[:], in_=w2_raw[:].rearrange("p r m o -> p r o m"))
@@ -165,20 +122,61 @@ def tile_infovae_pa_kernel(
             in_=w2_grouped[:].rearrange("p r o m -> p (r o m)"),
         )
 
-        out_rows = (
-            out_0.rearrange("(p i) o -> p (i o)", i=B_TILES),
-            out_1.rearrange("(p i) o -> p (i o)", i=B_TILES),
-        )
+        x_codes = keep.tile([P, PASSES1, B], U32, align_bytes=64)
+        x_scales = keep.tile([P, PASSES1, B], U8, align_bytes=64)
+        w1_codes = keep.tile([P, 2, PASSES1, H1], U32, align_bytes=64)
+        w1_scales = keep.tile([P, 2, PASSES1, H1], U8, align_bytes=64)
 
-        def hidden_layer(c, r):
+        def interleave_w1(r, g):
+            w1_grouped = stage.tile([P, H1, PACK], BF16, align_bytes=64, tag="w1_grouped")
+            v = W1_VECTOR_COLS
+            interleave_rows(nc.vector.tensor_copy, w1_grouped[:, :v, :], w1_raw[:, r, g, :, :v])
+            interleave_rows(nc.scalar.copy, w1_grouped[:, v:, :], w1_raw[:, r, g, :, v:])
+            return w1_grouped
+
+        def quantise_w1(r, g, w1_grouped):
+            nc.vector.quantize_mx(
+                out=w1_codes[:, r, g, :].bitcast(FP8X4),
+                scales=w1_scales[:, r, g, :],
+                in_=w1_grouped[:].rearrange("p c t -> p (c t)"),
+            )
+
+        def transpose_x(j):
+            banks = []
+            for g in range(PASSES1):
+                xt = psum_t.tile([P, 2, PAIR_COLS], F32, tag="xt")
+                for ii in range(2):
+                    words = x_sb[:, 2 * j + ii, :].bitcast(F32)
+                    for u in range(2):
+                        first = (K_PASS * g + 2 * P * u) // 2
+                        nc.tensor.transpose(
+                            xt[:, u, P * ii : P * (ii + 1)], words[:, first : first + P], ident[:]
+                        )
+                banks.append(xt)
+            return banks
+
+        def quantise_x(j, banks):
+            cols = slice(PAIR_COLS * j, PAIR_COLS * (j + 1))
+            for g in range(PASSES1):
+                x_grouped = stage.tile([P, PAIR_COLS * PACK], BF16, align_bytes=64, tag="x_grouped")
+                nc.scalar.copy(
+                    out=x_grouped[:].bitcast(F32).rearrange("p (b u) -> p b u", u=2),
+                    in_=banks[g][:].rearrange("p u b -> p b u"),
+                )
+                nc.vector.quantize_mx(
+                    out=x_codes[:, g, cols].bitcast(FP8X4), scales=x_scales[:, g, cols], in_=x_grouped[:]
+                )
+
+        def layer1(c, r):
             cols = slice(CHUNK_COLS * c, CHUNK_COLS * (c + 1))
-            planes = stage.tile([P, H_TILES, CHUNK_COLS], BF16 if r == SIG else F32, tag="planes%d" % r)
+            banks = []
             for m in range(H_TILES):
                 units = slice(P * m, P * (m + 1))
-                acc = psum_h.tile([P, CHUNK_COLS], F32, tag="acc")
+                if m % 2 == 0:
+                    banks.append(psum_h.tile([P, 2, CHUNK_COLS], F32, tag="bank", name="bank"))
                 for g in range(PASSES1):
                     nc.tensor.matmul_mx(
-                        out=acc[:],
+                        out=banks[m // 2][:, m % 2, :],
                         lhsT=w1_codes[:, r, g, units].bitcast(FP8X4),
                         lhsT_scale=w1_scales[:, r, g, units],
                         rhs=x_codes[:, g, cols].bitcast(FP8X4),
@@ -186,13 +184,21 @@ def tile_infovae_pa_kernel(
                         start=(g == 0),
                         stop=(g == PASSES1 - 1),
                     )
+            return banks
+
+        def activate(r, banks):
+            planes = stage.tile([P, H_TILES, CHUNK_COLS], BF16 if r == SIG else F32, tag="planes%d" % r)
+            for m in range(H_TILES):
                 nc.scalar.activation(
                     out=planes[:, m, :],
-                    in_=acc[:],
+                    in_=banks[m // 2][:, m % 2, :],
                     func=ACT.Tanh if r == SIG else ACT.Identity,
                     bias=b1_col[:, H_TILES * r + m : H_TILES * r + m + 1],
                     scale=1.0,
                 )
+            return planes
+
+        def interleave_h(r, planes):
             h_grouped = stage.tile([P, CHUNK_COLS, PACK], BF16, align_bytes=64, tag="h_grouped%d" % r)
             if r == SIG:
                 interleave_rows(nc.scalar.copy, h_grouped[:], planes[:])
@@ -201,14 +207,14 @@ def tile_infovae_pa_kernel(
                 nc.vector.scalar_tensor_tensor(
                     out=h_grouped[:], in0=by_column, scalar=NEG_SLOPE, in1=by_column, op0=ALU.mult, op1=ALU.max
                 )
+            return h_grouped
+
+        def layer2(r, h_grouped):
             h_codes = stage.tile([P, CHUNK_COLS], U32, align_bytes=64, tag="h_codes%d" % r)
             h_scales = stage.tile([P, CHUNK_COLS], U8, align_bytes=64, tag="h_scales%d" % r)
             nc.vector.quantize_mx(
                 out=h_codes[:].bitcast(FP8X4), scales=h_scales[:], in_=h_grouped[:].rearrange("p b m -> p (b m)")
             )
-            return h_codes, h_scales
-
-        def output_layer(r, h_codes, h_scales):
             outs = slice(H2 * r, H2 * (r + 1))
             acc = psum_o.tile([P, CHUNK_TILES, H2], F32, tag="out%d" % r)
             for i in range(CHUNK_TILES):
@@ -222,6 +228,10 @@ def tile_infovae_pa_kernel(
                     start=True,
                     stop=True,
                 )
+            return acc
+
+        def lrelu_biased(r, acc):
+            outs = slice(H2 * r, H2 * (r + 1))
             biased = stage.tile([P, CHUNK_TILES, H2], F32, tag="biased%d" % r)
             nc.vector.tensor_tensor(
                 out=biased[:],
@@ -236,19 +246,24 @@ def tile_infovae_pa_kernel(
             )
             return result
 
-        for c in range(CHUNKS):
-            cols = slice(CHUNK_COLS * c, CHUNK_COLS * (c + 1))
-            sig_codes, sig_scales = hidden_layer(c, SIG)
-            mu_codes, mu_scales = hidden_layer(c, MU)
-
-            log_var = output_layer(SIG, sig_codes, sig_scales)
+        def clipped(log_var):
             nc.vector.tensor_scalar(
                 out=log_var[:], in0=log_var[:], scalar1=LV_MAX, scalar2=LV_MIN, op0=ALU.min, op1=ALU.max
             )
+            return log_var
+
+        def exp_half(log_var):
             std = stage.tile([P, CHUNK_COLS], F32, tag="std")
             nc.scalar.activation(out=std[:], in_=log_var[:], func=ACT.Exp, scale=0.5)
-            mean = output_layer(MU, mu_codes, mu_scales)
+            return std
 
+        out_rows = (
+            out_0.rearrange("(p i) o -> p (i o)", i=B_TILES),
+            out_1.rearrange("(p i) o -> p (i o)", i=B_TILES),
+        )
+
+        def samples(c, mean, std):
+            cols = slice(CHUNK_COLS * c, CHUNK_COLS * (c + 1))
             both = [P, 2, CHUNK_COLS]
             z = stage.tile(both, F32, tag="z")
             nc.vector.tensor_tensor(
@@ -259,3 +274,40 @@ def tile_infovae_pa_kernel(
             )
             for n in range(2):
                 nc.sync.dma_start(out=out_rows[n][:, cols], in_=z[:, n, :])
+
+        grouped = interleave_w1(SIG, 0)
+        xt_next = transpose_x(0)
+        quantise_w1(SIG, 0, grouped)
+        grouped = interleave_w1(SIG, 1)
+        quantise_x(0, xt_next)
+        quantise_w1(SIG, 1, grouped)
+        banks_sig = layer1(0, SIG)
+        for g in range(PASSES1):
+            quantise_w1(MU, g, interleave_w1(MU, g))
+        xt_next = transpose_x(1)
+        banks_mu = layer1(0, MU)
+        planes_sig = activate(SIG, banks_sig)
+        quantise_x(1, xt_next)
+
+        for c in range(CHUNKS + 1):
+            if 0 < c < CHUNKS:
+                planes_sig = activate(SIG, banks_sig)
+            if c > 0:
+                std = exp_half(log_var)
+            if c < CHUNKS:
+                grouped_sig = interleave_h(SIG, planes_sig)
+                if c + 1 < CHUNKS:
+                    banks_sig = layer1(c + 1, SIG)
+                acc_sig = layer2(SIG, grouped_sig)
+            if c > 0:
+                samples(c - 1, lrelu_biased(MU, acc_mu), std)
+            if c + 2 < CHUNKS:
+                xt_next = transpose_x(c + 2)
+            if c < CHUNKS:
+                planes_mu = activate(MU, banks_mu)
+                if c + 1 < CHUNKS:
+                    banks_mu = layer1(c + 1, MU)
+                log_var = clipped(lrelu_biased(SIG, acc_sig))
+                acc_mu = layer2(MU, interleave_h(MU, planes_mu))
+            if c + 2 < CHUNKS:
+                quantise_x(c + 2, xt_next)

@@ -23,11 +23,11 @@ B_TILES = B // P
 PAIRS = B_TILES // 2
 PAIR_COLS = 2 * P
 PASSES1 = H0 // K_PASS
+W1_SCALAR_COLS = 192
 H_TILES = H1 // P
 CHUNKS = PAIRS
 CHUNK_TILES = B_TILES // CHUNKS
 CHUNK_COLS = CHUNK_TILES * P
-W1_VECTOR_COLS = 320
 
 MU, SIG = 0, 1
 
@@ -55,7 +55,7 @@ def tile_infovae_pa_kernel(
         stage = ctx.enter_context(tc.tile_pool(name="stage", bufs=3))
         psum_t = ctx.enter_context(tc.psum_pool(name="psum_t", bufs=2))
         psum_h = ctx.enter_context(tc.psum_pool(name="psum_h", bufs=4))
-        psum_o = ctx.enter_context(tc.psum_pool(name="psum_o", bufs=1))
+        psum_o = ctx.enter_context(tc.psum_pool(name="psum_o", bufs=2))
 
         ident = keep.tile([P, P], F32)
         make_identity(nc, ident[:])
@@ -89,15 +89,16 @@ def tile_infovae_pa_kernel(
                 in_=w1[r][K_PASS * g : K_PASS * (g + 1), :].rearrange("(u p e) c -> p u (e c)", u=2, e=2),
             )
 
-        for r in (MU, SIG):
-            nc.sync.dma_start(out=w2_raw[:, r], in_=w2[r].rearrange("(m p) o -> p m o", p=P))
         load_w1(SIG, 0)
         load_x_pair(0)
         load_w1(SIG, 1)
+        load_x_pair(1)
+        load_x_pair(2)
         load_w1(MU, 0)
         load_w1(MU, 1)
-        for j in range(1, PAIRS):
-            load_x_pair(j)
+        for r in (MU, SIG):
+            nc.sync.dma_start(out=w2_raw[:, r], in_=w2[r].rearrange("(m p) o -> p m o", p=P))
+        load_x_pair(3)
         nc.sync.dma_start(out=noise[:, 0, :], in_=noise_enc.rearrange("(p i) o -> p (i o)", i=B_TILES))
         nc.sync.dma_start(out=noise[:, 1, :], in_=noise_z.rearrange("(p i) o -> p (i o)", i=B_TILES))
 
@@ -109,32 +110,19 @@ def tile_infovae_pa_kernel(
         nc.vector.tensor_copy(out=b1_col[:], in_=b1_ps[:, 0 : 2 * H_TILES])
         b2_ps = psum_t.tile([P, 2 * H2], F32, tag="xt")
         nc.tensor.matmul(b2_ps[:], lhsT=ones[:], rhs=b2_rows[:], start=True, stop=True)
-        b2_all = keep.tile([P, 2 * H2], F32)
-        nc.vector.tensor_copy(out=b2_all[:], in_=b2_ps[:])
+        b2_all = keep.tile([P, 2, H2], F32)
+        nc.vector.tensor_copy(out=b2_all[:].rearrange("p r o -> p (r o)"), in_=b2_ps[:])
 
-        w2_grouped = keep.tile([P, 2, H2, PACK], BF16, align_bytes=64)
-        nc.vector.tensor_copy(out=w2_grouped[:], in_=w2_raw[:].rearrange("p r m o -> p r o m"))
-        w2_codes = keep.tile([P, 2 * H2], U32, align_bytes=64)
-        w2_scales = keep.tile([P, 2 * H2], U8, align_bytes=64)
-        nc.vector.quantize_mx(
-            out=w2_codes[:].bitcast(FP8X4),
-            scales=w2_scales[:],
-            in_=w2_grouped[:].rearrange("p r o m -> p (r o m)"),
-        )
-
-        x_codes = keep.tile([P, PASSES1, B], U32, align_bytes=64)
-        x_scales = keep.tile([P, PASSES1, B], U8, align_bytes=64)
+        x_codes = keep.tile([P, PAIRS, PASSES1, PAIR_COLS], U32, align_bytes=64)
+        x_scales = keep.tile([P, PAIRS, PASSES1, PAIR_COLS], U8, align_bytes=64)
         w1_codes = keep.tile([P, 2, PASSES1, H1], U32, align_bytes=64)
         w1_scales = keep.tile([P, 2, PASSES1, H1], U8, align_bytes=64)
 
-        def interleave_w1(r, g):
+        def quantise_w1(r, g):
             w1_grouped = stage.tile([P, H1, PACK], BF16, align_bytes=64, tag="w1_grouped")
-            v = W1_VECTOR_COLS
+            v = H1 - W1_SCALAR_COLS
             interleave_rows(nc.vector.tensor_copy, w1_grouped[:, :v, :], w1_raw[:, r, g, :, :v])
             interleave_rows(nc.scalar.copy, w1_grouped[:, v:, :], w1_raw[:, r, g, :, v:])
-            return w1_grouped
-
-        def quantise_w1(r, g, w1_grouped):
             nc.vector.quantize_mx(
                 out=w1_codes[:, r, g, :].bitcast(FP8X4),
                 scales=w1_scales[:, r, g, :],
@@ -156,19 +144,19 @@ def tile_infovae_pa_kernel(
             return banks
 
         def quantise_x(j, banks):
-            cols = slice(PAIR_COLS * j, PAIR_COLS * (j + 1))
+            x_grouped = stage.tile([P, PASSES1, PAIR_COLS * PACK], BF16, align_bytes=64, tag="x_grouped")
             for g in range(PASSES1):
-                x_grouped = stage.tile([P, PAIR_COLS * PACK], BF16, align_bytes=64, tag="x_grouped")
                 nc.scalar.copy(
-                    out=x_grouped[:].bitcast(F32).rearrange("p (b u) -> p b u", u=2),
+                    out=x_grouped[:, g, :].bitcast(F32).rearrange("p (b u) -> p b u", u=2),
                     in_=banks[g][:].rearrange("p u b -> p b u"),
                 )
-                nc.vector.quantize_mx(
-                    out=x_codes[:, g, cols].bitcast(FP8X4), scales=x_scales[:, g, cols], in_=x_grouped[:]
-                )
+            nc.vector.quantize_mx(
+                out=x_codes[:, j].rearrange("p g b -> p (g b)").bitcast(FP8X4),
+                scales=x_scales[:, j].rearrange("p g b -> p (g b)"),
+                in_=x_grouped[:].rearrange("p g b -> p (g b)"),
+            )
 
         def layer1(c, r):
-            cols = slice(CHUNK_COLS * c, CHUNK_COLS * (c + 1))
             banks = []
             for m in range(H_TILES):
                 units = slice(P * m, P * (m + 1))
@@ -179,8 +167,8 @@ def tile_infovae_pa_kernel(
                         out=banks[m // 2][:, m % 2, :],
                         lhsT=w1_codes[:, r, g, units].bitcast(FP8X4),
                         lhsT_scale=w1_scales[:, r, g, units],
-                        rhs=x_codes[:, g, cols].bitcast(FP8X4),
-                        rhs_scale=x_scales[:, g, cols],
+                        rhs=x_codes[:, c, g, :].bitcast(FP8X4),
+                        rhs_scale=x_scales[:, c, g, :],
                         start=(g == 0),
                         stop=(g == PASSES1 - 1),
                     )
@@ -209,18 +197,17 @@ def tile_infovae_pa_kernel(
                 )
             return h_grouped
 
-        def layer2(r, h_grouped):
+        def layer2(r, h_grouped, acc):
             h_codes = stage.tile([P, CHUNK_COLS], U32, align_bytes=64, tag="h_codes%d" % r)
             h_scales = stage.tile([P, CHUNK_COLS], U8, align_bytes=64, tag="h_scales%d" % r)
             nc.vector.quantize_mx(
                 out=h_codes[:].bitcast(FP8X4), scales=h_scales[:], in_=h_grouped[:].rearrange("p b m -> p (b m)")
             )
             outs = slice(H2 * r, H2 * (r + 1))
-            acc = psum_o.tile([P, CHUNK_TILES, H2], F32, tag="out%d" % r)
             for i in range(CHUNK_TILES):
                 rows = slice(P * i, P * (i + 1))
                 nc.tensor.matmul_mx(
-                    out=acc[:, i, :],
+                    out=acc[:, r, i, :],
                     lhsT=h_codes[:, rows].bitcast(FP8X4),
                     lhsT_scale=h_scales[:, rows],
                     rhs=w2_codes[:, outs].bitcast(FP8X4),
@@ -228,33 +215,36 @@ def tile_infovae_pa_kernel(
                     start=True,
                     stop=True,
                 )
-            return acc
 
-        def lrelu_biased(r, acc):
-            outs = slice(H2 * r, H2 * (r + 1))
-            biased = stage.tile([P, CHUNK_TILES, H2], F32, tag="biased%d" % r)
+        def lrelu_biased(acc, first, last):
+            branches = slice(first, last + 1)
+            n = last + 1 - first
+            biased = stage.tile([P, 2, CHUNK_TILES, H2], F32, tag="biased")
             nc.vector.tensor_tensor(
-                out=biased[:],
-                in0=acc[:],
-                in1=b2_all[:, outs].unsqueeze(1).to_broadcast([P, CHUNK_TILES, H2]),
+                out=biased[:, branches],
+                in0=acc[:, branches],
+                in1=b2_all[:, branches].unsqueeze(2).to_broadcast([P, n, CHUNK_TILES, H2]),
                 op=ALU.add,
             )
-            flat = biased[:].rearrange("p i o -> p (i o)")
-            result = stage.tile([P, CHUNK_COLS], F32, tag="lrelu%d" % r)
+            flat = biased[:, branches].rearrange("p r i o -> p (r i o)")
+            result = stage.tile([P, 2, CHUNK_COLS], F32, tag="lrelu")
             nc.vector.scalar_tensor_tensor(
-                out=result[:], in0=flat, scalar=NEG_SLOPE, in1=flat, op0=ALU.mult, op1=ALU.max
+                out=result[:, branches].rearrange("p r b -> p (r b)"),
+                in0=flat,
+                scalar=NEG_SLOPE,
+                in1=flat,
+                op0=ALU.mult,
+                op1=ALU.max,
             )
             return result
 
-        def clipped(log_var):
+        def exp_half_clipped(log_var):
+            clip = stage.tile([P, CHUNK_COLS], F32, tag="clip")
             nc.vector.tensor_scalar(
-                out=log_var[:], in0=log_var[:], scalar1=LV_MAX, scalar2=LV_MIN, op0=ALU.min, op1=ALU.max
+                out=clip[:], in0=log_var, scalar1=LV_MAX, scalar2=LV_MIN, op0=ALU.min, op1=ALU.max
             )
-            return log_var
-
-        def exp_half(log_var):
             std = stage.tile([P, CHUNK_COLS], F32, tag="std")
-            nc.scalar.activation(out=std[:], in_=log_var[:], func=ACT.Exp, scale=0.5)
+            nc.scalar.activation(out=std[:], in_=clip[:], func=ACT.Exp, scale=0.5)
             return std
 
         out_rows = (
@@ -270,44 +260,40 @@ def tile_infovae_pa_kernel(
                 out=z[:], in0=noise[:, :, cols], in1=std[:].unsqueeze(1).to_broadcast(both), op=ALU.mult
             )
             nc.vector.tensor_tensor(
-                out=z[:], in0=z[:], in1=mean[:].unsqueeze(1).to_broadcast(both), op=ALU.add
+                out=z[:], in0=z[:], in1=mean.unsqueeze(1).to_broadcast(both), op=ALU.add
             )
             for n in range(2):
                 nc.sync.dma_start(out=out_rows[n][:, cols], in_=z[:, n, :])
 
-        grouped = interleave_w1(SIG, 0)
-        xt_next = transpose_x(0)
-        quantise_w1(SIG, 0, grouped)
-        grouped = interleave_w1(SIG, 1)
-        quantise_x(0, xt_next)
-        quantise_w1(SIG, 1, grouped)
-        banks_sig = layer1(0, SIG)
-        for g in range(PASSES1):
-            quantise_w1(MU, g, interleave_w1(MU, g))
-        xt_next = transpose_x(1)
-        banks_mu = layer1(0, MU)
-        planes_sig = activate(SIG, banks_sig)
-        quantise_x(1, xt_next)
+        quantise_w1(SIG, 0)
+        quantise_x(0, transpose_x(0))
+        quantise_w1(SIG, 1)
+        quantise_x(1, transpose_x(1))
+        quantise_x(2, transpose_x(2))
+        quantise_w1(MU, 0)
+        quantise_w1(MU, 1)
 
+        w2_grouped = keep.tile([P, 2, H2, PACK], BF16, align_bytes=64)
+        nc.vector.tensor_copy(out=w2_grouped[:], in_=w2_raw[:].rearrange("p r m o -> p r o m"))
+        w2_codes = keep.tile([P, 2 * H2], U32, align_bytes=64)
+        w2_scales = keep.tile([P, 2 * H2], U8, align_bytes=64)
+        nc.vector.quantize_mx(
+            out=w2_codes[:].bitcast(FP8X4),
+            scales=w2_scales[:],
+            in_=w2_grouped[:].rearrange("p r o m -> p (r o m)"),
+        )
+
+        std = {}
         for c in range(CHUNKS + 1):
-            if 0 < c < CHUNKS:
-                planes_sig = activate(SIG, banks_sig)
-            if c > 0:
-                std = exp_half(log_var)
+            acc = psum_o.tile([P, 2, CHUNK_TILES, H2], F32, tag="out")
             if c < CHUNKS:
-                grouped_sig = interleave_h(SIG, planes_sig)
-                if c + 1 < CHUNKS:
-                    banks_sig = layer1(c + 1, SIG)
-                acc_sig = layer2(SIG, grouped_sig)
+                layer2(SIG, interleave_h(SIG, activate(SIG, layer1(c, SIG))), acc)
+            if c == 0:
+                quantise_x(3, transpose_x(3))
             if c > 0:
-                samples(c - 1, lrelu_biased(MU, acc_mu), std)
-            if c + 2 < CHUNKS:
-                xt_next = transpose_x(c + 2)
+                layer2(MU, interleave_h(MU, activate(MU, layer1(c - 1, MU))), acc)
+            result = lrelu_biased(acc, MU if c > 0 else SIG, SIG if c < CHUNKS else MU)
             if c < CHUNKS:
-                planes_mu = activate(MU, banks_mu)
-                if c + 1 < CHUNKS:
-                    banks_mu = layer1(c + 1, MU)
-                log_var = clipped(lrelu_biased(SIG, acc_sig))
-                acc_mu = layer2(MU, interleave_h(MU, planes_mu))
-            if c + 2 < CHUNKS:
-                quantise_x(c + 2, xt_next)
+                std[c] = exp_half_clipped(result[:, SIG, :])
+            if c > 0:
+                samples(c - 1, result[:, MU, :], std[c - 1])

@@ -23,11 +23,11 @@ B_TILES = B // P
 PAIRS = B_TILES // 2
 PAIR_COLS = 2 * P
 PASSES1 = H0 // K_PASS
-W1_SCALAR_COLS = 192
 H_TILES = H1 // P
 CHUNKS = PAIRS
 CHUNK_TILES = B_TILES // CHUNKS
 CHUNK_COLS = CHUNK_TILES * P
+W1_VECTOR_COLS = 416
 
 MU, SIG = 0, 1
 
@@ -55,7 +55,7 @@ def tile_infovae_pa_kernel(
         stage = ctx.enter_context(tc.tile_pool(name="stage", bufs=3))
         psum_t = ctx.enter_context(tc.psum_pool(name="psum_t", bufs=2))
         psum_h = ctx.enter_context(tc.psum_pool(name="psum_h", bufs=4))
-        psum_o = ctx.enter_context(tc.psum_pool(name="psum_o", bufs=2))
+        psum_o = ctx.enter_context(tc.psum_pool(name="psum_o", bufs=1))
 
         ident = keep.tile([P, P], F32)
         make_identity(nc, ident[:])
@@ -89,16 +89,15 @@ def tile_infovae_pa_kernel(
                 in_=w1[r][K_PASS * g : K_PASS * (g + 1), :].rearrange("(u p e) c -> p u (e c)", u=2, e=2),
             )
 
+        for r in (MU, SIG):
+            nc.sync.dma_start(out=w2_raw[:, r], in_=w2[r].rearrange("(m p) o -> p m o", p=P))
         load_w1(SIG, 0)
         load_x_pair(0)
         load_w1(SIG, 1)
-        load_x_pair(1)
-        load_x_pair(2)
         load_w1(MU, 0)
         load_w1(MU, 1)
-        for r in (MU, SIG):
-            nc.sync.dma_start(out=w2_raw[:, r], in_=w2[r].rearrange("(m p) o -> p m o", p=P))
-        load_x_pair(3)
+        for j in range(1, PAIRS):
+            load_x_pair(j)
         nc.sync.dma_start(out=noise[:, 0, :], in_=noise_enc.rearrange("(p i) o -> p (i o)", i=B_TILES))
         nc.sync.dma_start(out=noise[:, 1, :], in_=noise_z.rearrange("(p i) o -> p (i o)", i=B_TILES))
 
@@ -110,19 +109,32 @@ def tile_infovae_pa_kernel(
         nc.vector.tensor_copy(out=b1_col[:], in_=b1_ps[:, 0 : 2 * H_TILES])
         b2_ps = psum_t.tile([P, 2 * H2], F32, tag="xt")
         nc.tensor.matmul(b2_ps[:], lhsT=ones[:], rhs=b2_rows[:], start=True, stop=True)
-        b2_all = keep.tile([P, 2, H2], F32)
-        nc.vector.tensor_copy(out=b2_all[:].rearrange("p r o -> p (r o)"), in_=b2_ps[:])
+        b2_all = keep.tile([P, 2 * H2], F32)
+        nc.vector.tensor_copy(out=b2_all[:], in_=b2_ps[:])
 
-        x_codes = keep.tile([P, PAIRS, PASSES1, PAIR_COLS], U32, align_bytes=64)
-        x_scales = keep.tile([P, PAIRS, PASSES1, PAIR_COLS], U8, align_bytes=64)
+        w2_grouped = keep.tile([P, 2, H2, PACK], BF16, align_bytes=64)
+        nc.vector.tensor_copy(out=w2_grouped[:], in_=w2_raw[:].rearrange("p r m o -> p r o m"))
+        w2_codes = keep.tile([P, 2 * H2], U32, align_bytes=64)
+        w2_scales = keep.tile([P, 2 * H2], U8, align_bytes=64)
+        nc.vector.quantize_mx(
+            out=w2_codes[:].bitcast(FP8X4),
+            scales=w2_scales[:],
+            in_=w2_grouped[:].rearrange("p r o m -> p (r o m)"),
+        )
+
+        x_codes = keep.tile([P, PASSES1, B], U32, align_bytes=64)
+        x_scales = keep.tile([P, PASSES1, B], U8, align_bytes=64)
         w1_codes = keep.tile([P, 2, PASSES1, H1], U32, align_bytes=64)
         w1_scales = keep.tile([P, 2, PASSES1, H1], U8, align_bytes=64)
 
-        def quantise_w1(r, g):
+        def interleave_w1(r, g):
             w1_grouped = stage.tile([P, H1, PACK], BF16, align_bytes=64, tag="w1_grouped")
-            v = H1 - W1_SCALAR_COLS
+            v = W1_VECTOR_COLS
             interleave_rows(nc.vector.tensor_copy, w1_grouped[:, :v, :], w1_raw[:, r, g, :, :v])
             interleave_rows(nc.scalar.copy, w1_grouped[:, v:, :], w1_raw[:, r, g, :, v:])
+            return w1_grouped
+
+        def quantise_w1(r, g, w1_grouped):
             nc.vector.quantize_mx(
                 out=w1_codes[:, r, g, :].bitcast(FP8X4),
                 scales=w1_scales[:, r, g, :],
@@ -144,19 +156,19 @@ def tile_infovae_pa_kernel(
             return banks
 
         def quantise_x(j, banks):
-            x_grouped = stage.tile([P, PASSES1, PAIR_COLS * PACK], BF16, align_bytes=64, tag="x_grouped")
+            cols = slice(PAIR_COLS * j, PAIR_COLS * (j + 1))
             for g in range(PASSES1):
+                x_grouped = stage.tile([P, PAIR_COLS * PACK], BF16, align_bytes=64, tag="x_grouped")
                 nc.scalar.copy(
-                    out=x_grouped[:, g, :].bitcast(F32).rearrange("p (b u) -> p b u", u=2),
+                    out=x_grouped[:].bitcast(F32).rearrange("p (b u) -> p b u", u=2),
                     in_=banks[g][:].rearrange("p u b -> p b u"),
                 )
-            nc.vector.quantize_mx(
-                out=x_codes[:, j].rearrange("p g b -> p (g b)").bitcast(FP8X4),
-                scales=x_scales[:, j].rearrange("p g b -> p (g b)"),
-                in_=x_grouped[:].rearrange("p g b -> p (g b)"),
-            )
+                nc.vector.quantize_mx(
+                    out=x_codes[:, g, cols].bitcast(FP8X4), scales=x_scales[:, g, cols], in_=x_grouped[:]
+                )
 
         def layer1(c, r):
+            cols = slice(CHUNK_COLS * c, CHUNK_COLS * (c + 1))
             banks = []
             for m in range(H_TILES):
                 units = slice(P * m, P * (m + 1))
@@ -167,8 +179,8 @@ def tile_infovae_pa_kernel(
                         out=banks[m // 2][:, m % 2, :],
                         lhsT=w1_codes[:, r, g, units].bitcast(FP8X4),
                         lhsT_scale=w1_scales[:, r, g, units],
-                        rhs=x_codes[:, c, g, :].bitcast(FP8X4),
-                        rhs_scale=x_scales[:, c, g, :],
+                        rhs=x_codes[:, g, cols].bitcast(FP8X4),
+                        rhs_scale=x_scales[:, g, cols],
                         start=(g == 0),
                         stop=(g == PASSES1 - 1),
                     )
@@ -197,17 +209,18 @@ def tile_infovae_pa_kernel(
                 )
             return h_grouped
 
-        def layer2(r, h_grouped, acc):
+        def layer2(r, h_grouped):
             h_codes = stage.tile([P, CHUNK_COLS], U32, align_bytes=64, tag="h_codes%d" % r)
             h_scales = stage.tile([P, CHUNK_COLS], U8, align_bytes=64, tag="h_scales%d" % r)
             nc.vector.quantize_mx(
                 out=h_codes[:].bitcast(FP8X4), scales=h_scales[:], in_=h_grouped[:].rearrange("p b m -> p (b m)")
             )
             outs = slice(H2 * r, H2 * (r + 1))
+            acc = psum_o.tile([P, CHUNK_TILES, H2], F32, tag="out%d" % r)
             for i in range(CHUNK_TILES):
                 rows = slice(P * i, P * (i + 1))
                 nc.tensor.matmul_mx(
-                    out=acc[:, r, i, :],
+                    out=acc[:, i, :],
                     lhsT=h_codes[:, rows].bitcast(FP8X4),
                     lhsT_scale=h_scales[:, rows],
                     rhs=w2_codes[:, outs].bitcast(FP8X4),
@@ -215,36 +228,33 @@ def tile_infovae_pa_kernel(
                     start=True,
                     stop=True,
                 )
+            return acc
 
-        def lrelu_biased(acc, first, last):
-            branches = slice(first, last + 1)
-            n = last + 1 - first
-            biased = stage.tile([P, 2, CHUNK_TILES, H2], F32, tag="biased")
+        def lrelu_biased(r, acc):
+            outs = slice(H2 * r, H2 * (r + 1))
+            biased = stage.tile([P, CHUNK_TILES, H2], F32, tag="biased%d" % r)
             nc.vector.tensor_tensor(
-                out=biased[:, branches],
-                in0=acc[:, branches],
-                in1=b2_all[:, branches].unsqueeze(2).to_broadcast([P, n, CHUNK_TILES, H2]),
+                out=biased[:],
+                in0=acc[:],
+                in1=b2_all[:, outs].unsqueeze(1).to_broadcast([P, CHUNK_TILES, H2]),
                 op=ALU.add,
             )
-            flat = biased[:, branches].rearrange("p r i o -> p (r i o)")
-            result = stage.tile([P, 2, CHUNK_COLS], F32, tag="lrelu")
+            flat = biased[:].rearrange("p i o -> p (i o)")
+            result = stage.tile([P, CHUNK_COLS], F32, tag="lrelu%d" % r)
             nc.vector.scalar_tensor_tensor(
-                out=result[:, branches].rearrange("p r b -> p (r b)"),
-                in0=flat,
-                scalar=NEG_SLOPE,
-                in1=flat,
-                op0=ALU.mult,
-                op1=ALU.max,
+                out=result[:], in0=flat, scalar=NEG_SLOPE, in1=flat, op0=ALU.mult, op1=ALU.max
             )
             return result
 
-        def exp_half_clipped(log_var):
-            clip = stage.tile([P, CHUNK_COLS], F32, tag="clip")
+        def clipped(log_var):
             nc.vector.tensor_scalar(
-                out=clip[:], in0=log_var, scalar1=LV_MAX, scalar2=LV_MIN, op0=ALU.min, op1=ALU.max
+                out=log_var[:], in0=log_var[:], scalar1=LV_MAX, scalar2=LV_MIN, op0=ALU.min, op1=ALU.max
             )
+            return log_var
+
+        def exp_half(log_var):
             std = stage.tile([P, CHUNK_COLS], F32, tag="std")
-            nc.scalar.activation(out=std[:], in_=clip[:], func=ACT.Exp, scale=0.5)
+            nc.scalar.activation(out=std[:], in_=log_var[:], func=ACT.Exp, scale=0.5)
             return std
 
         out_rows = (
@@ -260,40 +270,44 @@ def tile_infovae_pa_kernel(
                 out=z[:], in0=noise[:, :, cols], in1=std[:].unsqueeze(1).to_broadcast(both), op=ALU.mult
             )
             nc.vector.tensor_tensor(
-                out=z[:], in0=z[:], in1=mean.unsqueeze(1).to_broadcast(both), op=ALU.add
+                out=z[:], in0=z[:], in1=mean[:].unsqueeze(1).to_broadcast(both), op=ALU.add
             )
             for n in range(2):
                 nc.sync.dma_start(out=out_rows[n][:, cols], in_=z[:, n, :])
 
-        quantise_w1(SIG, 0)
-        quantise_x(0, transpose_x(0))
-        quantise_w1(SIG, 1)
-        quantise_x(1, transpose_x(1))
-        quantise_x(2, transpose_x(2))
-        quantise_w1(MU, 0)
-        quantise_w1(MU, 1)
+        grouped = interleave_w1(SIG, 0)
+        xt_next = transpose_x(0)
+        quantise_w1(SIG, 0, grouped)
+        grouped = interleave_w1(SIG, 1)
+        quantise_x(0, xt_next)
+        quantise_w1(SIG, 1, grouped)
+        banks_sig = layer1(0, SIG)
+        for g in range(PASSES1):
+            quantise_w1(MU, g, interleave_w1(MU, g))
+        xt_next = transpose_x(1)
+        banks_mu = layer1(0, MU)
+        planes_sig = activate(SIG, banks_sig)
+        quantise_x(1, xt_next)
 
-        w2_grouped = keep.tile([P, 2, H2, PACK], BF16, align_bytes=64)
-        nc.vector.tensor_copy(out=w2_grouped[:], in_=w2_raw[:].rearrange("p r m o -> p r o m"))
-        w2_codes = keep.tile([P, 2 * H2], U32, align_bytes=64)
-        w2_scales = keep.tile([P, 2 * H2], U8, align_bytes=64)
-        nc.vector.quantize_mx(
-            out=w2_codes[:].bitcast(FP8X4),
-            scales=w2_scales[:],
-            in_=w2_grouped[:].rearrange("p r o m -> p (r o m)"),
-        )
-
-        std = {}
         for c in range(CHUNKS + 1):
-            acc = psum_o.tile([P, 2, CHUNK_TILES, H2], F32, tag="out")
-            if c < CHUNKS:
-                layer2(SIG, interleave_h(SIG, activate(SIG, layer1(c, SIG))), acc)
-            if c == 0:
-                quantise_x(3, transpose_x(3))
+            if 0 < c < CHUNKS:
+                planes_sig = activate(SIG, banks_sig)
             if c > 0:
-                layer2(MU, interleave_h(MU, activate(MU, layer1(c - 1, MU))), acc)
-            result = lrelu_biased(acc, MU if c > 0 else SIG, SIG if c < CHUNKS else MU)
+                std = exp_half(log_var)
             if c < CHUNKS:
-                std[c] = exp_half_clipped(result[:, SIG, :])
+                grouped_sig = interleave_h(SIG, planes_sig)
+                if c + 1 < CHUNKS:
+                    banks_sig = layer1(c + 1, SIG)
+                acc_sig = layer2(SIG, grouped_sig)
             if c > 0:
-                samples(c - 1, result[:, MU, :], std[c - 1])
+                samples(c - 1, lrelu_biased(MU, acc_mu), std)
+            if c + 2 < CHUNKS:
+                xt_next = transpose_x(c + 2)
+            if c < CHUNKS:
+                planes_mu = activate(MU, banks_mu)
+                if c + 1 < CHUNKS:
+                    banks_mu = layer1(c + 1, MU)
+                log_var = clipped(lrelu_biased(SIG, acc_sig))
+                acc_mu = layer2(MU, interleave_h(MU, planes_mu))
+            if c + 2 < CHUNKS:
+                quantise_x(c + 2, xt_next)

@@ -27,7 +27,7 @@ H_TILES = H1 // P
 CHUNKS = PAIRS
 CHUNK_TILES = B_TILES // CHUNKS
 CHUNK_COLS = CHUNK_TILES * P
-W1_VECTOR_COLS = 416
+W1_VECTOR_COLS = 384
 
 MU, SIG = 0, 1
 
@@ -54,11 +54,15 @@ def tile_infovae_pa_kernel(
         keep = ctx.enter_context(tc.tile_pool(name="keep", bufs=1))
         stage = ctx.enter_context(tc.tile_pool(name="stage", bufs=3))
         psum_t = ctx.enter_context(tc.psum_pool(name="psum_t", bufs=2))
-        psum_h = ctx.enter_context(tc.psum_pool(name="psum_h", bufs=4))
+        psum_h = ctx.enter_context(tc.psum_pool(name="psum_h", bufs=2))
         psum_o = ctx.enter_context(tc.psum_pool(name="psum_o", bufs=1))
 
         ident = keep.tile([P, P], F32)
         make_identity(nc, ident[:])
+        ident_cols = keep.tile([P, 2 * H_TILES], BF16)
+        nc.gpsimd.tensor_copy(out=ident_cols[:], in_=ident[:, 0 : 2 * H_TILES])
+
+        ctx.enter_context(tc.manual_schedule())
 
         b1_rows = keep.tile([P, P], BF16)
         b2_rows = keep.tile([P, 2 * H2], BF16)
@@ -67,10 +71,10 @@ def tile_infovae_pa_kernel(
         nc.vector.memset(b2_rows[:], 0.0)
         nc.vector.memset(ones[:], 1.0)
         for r in (MU, SIG):
-            nc.sync.dma_start(
+            nc.scalar.dma_start(
                 out=b1_rows[H_TILES * r : H_TILES * (r + 1), :], in_=b1[r].rearrange("(m p) -> m p", p=P)
             )
-            nc.sync.dma_start(
+            nc.scalar.dma_start(
                 out=b2_rows[0:1, H2 * r : H2 * (r + 1)], in_=b2[r].rearrange("(a o) -> a o", a=1)
             )
 
@@ -78,7 +82,7 @@ def tile_infovae_pa_kernel(
         x_rows = x.rearrange("(p i) k -> p i k", i=B_TILES)
         w1_raw = keep.tile([P, 2, PASSES1, PACK, H1], BF16)
         w2_raw = keep.tile([P, 2, PACK, H2], BF16)
-        noise = keep.tile([P, 2, B_TILES * H2], BF16)
+        noise = keep.tile([P, 2, B_TILES, H2], BF16)
 
         def load_x_pair(j):
             nc.sync.dma_start(out=x_sb[:, 2 * j : 2 * j + 2, :], in_=x_rows[:, 2 * j : 2 * j + 2, :])
@@ -89,38 +93,40 @@ def tile_infovae_pa_kernel(
                 in_=w1[r][K_PASS * g : K_PASS * (g + 1), :].rearrange("(u p e) c -> p u (e c)", u=2, e=2),
             )
 
-        for r in (MU, SIG):
-            nc.sync.dma_start(out=w2_raw[:, r], in_=w2[r].rearrange("(m p) o -> p m o", p=P))
         load_w1(SIG, 0)
-        load_x_pair(0)
         load_w1(SIG, 1)
+        load_x_pair(0)
+        load_x_pair(1)
         load_w1(MU, 0)
         load_w1(MU, 1)
-        for j in range(1, PAIRS):
-            load_x_pair(j)
-        nc.sync.dma_start(out=noise[:, 0, :], in_=noise_enc.rearrange("(p i) o -> p (i o)", i=B_TILES))
-        nc.sync.dma_start(out=noise[:, 1, :], in_=noise_z.rearrange("(p i) o -> p (i o)", i=B_TILES))
+        for r in (SIG, MU):
+            nc.sync.dma_start(out=w2_raw[:, r], in_=w2[r].rearrange("(m p) o -> p m o", p=P))
+        load_x_pair(2)
+        load_x_pair(3)
+        nc.sync.dma_start(out=noise[:, 0], in_=noise_enc.rearrange("(p i) o -> p i o", i=B_TILES))
+        nc.sync.dma_start(out=noise[:, 1], in_=noise_z.rearrange("(p i) o -> p i o", i=B_TILES))
 
-        b1_rows_f32 = keep.tile([P, P], F32)
-        nc.vector.tensor_copy(out=b1_rows_f32[:], in_=b1_rows[:])
-        b1_ps = psum_t.tile([P, P], F32, tag="xt")
-        nc.tensor.transpose(b1_ps[:], b1_rows_f32[:], ident[:])
+        bias_ps = psum_o.tile([P, 2 * H2 + 2 * H_TILES], F32, tag="out0")
+        nc.tensor.matmul(bias_ps[:, 2 * H2 :], lhsT=b1_rows[:], rhs=ident_cols[:], start=True, stop=True)
+        nc.tensor.matmul(bias_ps[:, 0 : 2 * H2], lhsT=ones[:], rhs=b2_rows[:], start=True, stop=True)
         b1_col = keep.tile([P, 2 * H_TILES], F32)
-        nc.vector.tensor_copy(out=b1_col[:], in_=b1_ps[:, 0 : 2 * H_TILES])
-        b2_ps = psum_t.tile([P, 2 * H2], F32, tag="xt")
-        nc.tensor.matmul(b2_ps[:], lhsT=ones[:], rhs=b2_rows[:], start=True, stop=True)
+        nc.vector.tensor_copy(out=b1_col[:], in_=bias_ps[:, 2 * H2 :])
         b2_all = keep.tile([P, 2 * H2], F32)
-        nc.vector.tensor_copy(out=b2_all[:], in_=b2_ps[:])
+        nc.vector.tensor_copy(out=b2_all[:], in_=bias_ps[:, 0 : 2 * H2])
 
         w2_grouped = keep.tile([P, 2, H2, PACK], BF16, align_bytes=64)
-        nc.vector.tensor_copy(out=w2_grouped[:], in_=w2_raw[:].rearrange("p r m o -> p r o m"))
         w2_codes = keep.tile([P, 2 * H2], U32, align_bytes=64)
         w2_scales = keep.tile([P, 2 * H2], U8, align_bytes=64)
-        nc.vector.quantize_mx(
-            out=w2_codes[:].bitcast(FP8X4),
-            scales=w2_scales[:],
-            in_=w2_grouped[:].rearrange("p r o m -> p (r o m)"),
-        )
+
+        def interleave_w2(r):
+            nc.vector.tensor_copy(out=w2_grouped[:, r], in_=w2_raw[:, r].rearrange("p m o -> p o m"))
+
+        def quantise_w2():
+            nc.vector.quantize_mx(
+                out=w2_codes[:].bitcast(FP8X4),
+                scales=w2_scales[:],
+                in_=w2_grouped[:].rearrange("p r o m -> p (r o m)"),
+            )
 
         x_codes = keep.tile([P, PASSES1, B], U32, align_bytes=64)
         x_scales = keep.tile([P, PASSES1, B], U8, align_bytes=64)
@@ -155,17 +161,19 @@ def tile_infovae_pa_kernel(
                 banks.append(xt)
             return banks
 
-        def quantise_x(j, banks):
+        def copy_x(g, banks):
+            x_grouped = stage.tile([P, PAIR_COLS * PACK], BF16, align_bytes=64, tag="x_grouped")
+            nc.scalar.copy(
+                out=x_grouped[:].bitcast(F32).rearrange("p (b u) -> p b u", u=2),
+                in_=banks[g][:].rearrange("p u b -> p b u"),
+            )
+            return x_grouped
+
+        def quantise_x(j, g, x_grouped):
             cols = slice(PAIR_COLS * j, PAIR_COLS * (j + 1))
-            for g in range(PASSES1):
-                x_grouped = stage.tile([P, PAIR_COLS * PACK], BF16, align_bytes=64, tag="x_grouped")
-                nc.scalar.copy(
-                    out=x_grouped[:].bitcast(F32).rearrange("p (b u) -> p b u", u=2),
-                    in_=banks[g][:].rearrange("p u b -> p b u"),
-                )
-                nc.vector.quantize_mx(
-                    out=x_codes[:, g, cols].bitcast(FP8X4), scales=x_scales[:, g, cols], in_=x_grouped[:]
-                )
+            nc.vector.quantize_mx(
+                out=x_codes[:, g, cols].bitcast(FP8X4), scales=x_scales[:, g, cols], in_=x_grouped[:]
+            )
 
         def layer1(c, r):
             cols = slice(CHUNK_COLS * c, CHUNK_COLS * (c + 1))
@@ -173,7 +181,7 @@ def tile_infovae_pa_kernel(
             for m in range(H_TILES):
                 units = slice(P * m, P * (m + 1))
                 if m % 2 == 0:
-                    banks.append(psum_h.tile([P, 2, CHUNK_COLS], F32, tag="bank", name="bank"))
+                    banks.append(psum_h.tile([P, 2, CHUNK_COLS], F32, tag="bank%d" % r, name="bank"))
                 for g in range(PASSES1):
                     nc.tensor.matmul_mx(
                         out=banks[m // 2][:, m % 2, :],
@@ -198,15 +206,17 @@ def tile_infovae_pa_kernel(
                 )
             return planes
 
-        def interleave_h(r, planes):
-            h_grouped = stage.tile([P, CHUNK_COLS, PACK], BF16, align_bytes=64, tag="h_grouped%d" % r)
-            if r == SIG:
-                interleave_rows(nc.scalar.copy, h_grouped[:], planes[:])
-            else:
-                by_column = planes[:].rearrange("p m b -> p b m")
-                nc.vector.scalar_tensor_tensor(
-                    out=h_grouped[:], in0=by_column, scalar=NEG_SLOPE, in1=by_column, op0=ALU.mult, op1=ALU.max
-                )
+        def interleave_sig(copy, planes):
+            h_grouped = stage.tile([P, CHUNK_COLS, PACK], BF16, align_bytes=64, tag="h_grouped1")
+            interleave_rows(copy, h_grouped[:], planes[:])
+            return h_grouped
+
+        def lrelu_mu(planes):
+            h_grouped = stage.tile([P, CHUNK_COLS, PACK], BF16, align_bytes=64, tag="h_grouped0")
+            by_column = planes[:].rearrange("p m b -> p b m")
+            nc.vector.scalar_tensor_tensor(
+                out=h_grouped[:], in0=by_column, scalar=NEG_SLOPE, in1=by_column, op0=ALU.mult, op1=ALU.max
+            )
             return h_grouped
 
         def layer2(r, h_grouped):
@@ -230,84 +240,149 @@ def tile_infovae_pa_kernel(
                 )
             return acc
 
-        def lrelu_biased(r, acc):
-            outs = slice(H2 * r, H2 * (r + 1))
-            biased = stage.tile([P, CHUNK_TILES, H2], F32, tag="biased%d" % r)
+        whole = slice(0, CHUNK_TILES)
+
+        def add_b2(r, acc, biased, tiles=whole):
+            shape = [P, tiles.stop - tiles.start, H2]
             nc.vector.tensor_tensor(
-                out=biased[:],
-                in0=acc[:],
-                in1=b2_all[:, outs].unsqueeze(1).to_broadcast([P, CHUNK_TILES, H2]),
+                out=biased[:, tiles, :],
+                in0=acc[:, tiles, :],
+                in1=b2_all[:, H2 * r : H2 * (r + 1)].unsqueeze(1).to_broadcast(shape),
                 op=ALU.add,
             )
-            flat = biased[:].rearrange("p i o -> p (i o)")
-            result = stage.tile([P, CHUNK_COLS], F32, tag="lrelu%d" % r)
-            nc.vector.scalar_tensor_tensor(
-                out=result[:], in0=flat, scalar=NEG_SLOPE, in1=flat, op0=ALU.mult, op1=ALU.max
-            )
-            return result
 
-        def clipped(log_var):
+        def lrelu_out(biased, result, tiles=whole):
+            nc.vector.scalar_tensor_tensor(
+                out=result[:, tiles, :],
+                in0=biased[:, tiles, :],
+                scalar=NEG_SLOPE,
+                in1=biased[:, tiles, :],
+                op0=ALU.mult,
+                op1=ALU.max,
+            )
+
+        def out_tile(name):
+            return stage.tile([P, CHUNK_TILES, H2], F32, tag=name, name=name)
+
+        def clip(log_var):
             nc.vector.tensor_scalar(
                 out=log_var[:], in0=log_var[:], scalar1=LV_MAX, scalar2=LV_MIN, op0=ALU.min, op1=ALU.max
             )
-            return log_var
 
         def exp_half(log_var):
-            std = stage.tile([P, CHUNK_COLS], F32, tag="std")
+            std = out_tile("std")
             nc.scalar.activation(out=std[:], in_=log_var[:], func=ACT.Exp, scale=0.5)
             return std
 
         out_rows = (
-            out_0.rearrange("(p i) o -> p (i o)", i=B_TILES),
-            out_1.rearrange("(p i) o -> p (i o)", i=B_TILES),
+            out_0.rearrange("(p i) o -> p i o", i=B_TILES),
+            out_1.rearrange("(p i) o -> p i o", i=B_TILES),
         )
 
-        def samples(c, mean, std):
-            cols = slice(CHUNK_COLS * c, CHUNK_COLS * (c + 1))
-            both = [P, 2, CHUNK_COLS]
+        def scale_noise(c, std):
+            both = [P, 2, CHUNK_TILES, H2]
             z = stage.tile(both, F32, tag="z")
             nc.vector.tensor_tensor(
-                out=z[:], in0=noise[:, :, cols], in1=std[:].unsqueeze(1).to_broadcast(both), op=ALU.mult
+                out=z[:],
+                in0=noise[:, :, CHUNK_TILES * c : CHUNK_TILES * (c + 1), :],
+                in1=std[:].unsqueeze(1).to_broadcast(both),
+                op=ALU.mult,
             )
+            return z
+
+        def add_mean(c, z, mean, tiles=whole):
+            n_tiles = tiles.stop - tiles.start
             nc.vector.tensor_tensor(
-                out=z[:], in0=z[:], in1=mean[:].unsqueeze(1).to_broadcast(both), op=ALU.add
+                out=z[:, :, tiles, :],
+                in0=z[:, :, tiles, :],
+                in1=mean[:, tiles, :].unsqueeze(1).to_broadcast([P, 2, n_tiles, H2]),
+                op=ALU.add,
             )
+            first = CHUNK_TILES * c + tiles.start
             for n in range(2):
-                nc.sync.dma_start(out=out_rows[n][:, cols], in_=z[:, n, :])
+                nc.sync.dma_start(out=out_rows[n][:, first : first + n_tiles, :], in_=z[:, n, tiles, :])
 
-        grouped = interleave_w1(SIG, 0)
-        xt_next = transpose_x(0)
-        quantise_w1(SIG, 0, grouped)
-        grouped = interleave_w1(SIG, 1)
-        quantise_x(0, xt_next)
-        quantise_w1(SIG, 1, grouped)
-        banks_sig = layer1(0, SIG)
+        sig_raw = [interleave_w1(SIG, 0)]
+        xt = transpose_x(0)
+        sig_raw.append(interleave_w1(SIG, 1))
+        quantise_w1(SIG, 0, sig_raw[0])
+        x_raw = [copy_x(g, xt) for g in range(PASSES1)]
+        quantise_w1(SIG, 1, sig_raw[1])
         for g in range(PASSES1):
-            quantise_w1(MU, g, interleave_w1(MU, g))
-        xt_next = transpose_x(1)
-        banks_mu = layer1(0, MU)
+            quantise_x(0, g, x_raw[g])
+        xt = transpose_x(1)
+        banks_sig = layer1(0, SIG)
+        x_raw = [copy_x(g, xt) for g in range(PASSES1)]
+        mu_raw = interleave_w1(MU, 0)
         planes_sig = activate(SIG, banks_sig)
-        quantise_x(1, xt_next)
+        quantise_x(1, 0, x_raw[0])
+        quantise_w1(MU, 0, mu_raw)
+        quantise_x(1, 1, x_raw[1])
+        banks_sig = layer1(1, SIG)
+        xt = transpose_x(2)
+        mu_raw = interleave_w1(MU, 1)
+        interleave_w2(SIG)
+        quantise_w1(MU, 1, mu_raw)
+        interleave_w2(MU)
+        h_sig = interleave_sig(nc.vector.tensor_copy, planes_sig)
+        quantise_w2()
+        banks_mu = layer1(0, MU)
+        acc_sig = layer2(SIG, h_sig)
+        x_raw = [copy_x(0, xt)]
 
-        for c in range(CHUNKS + 1):
-            if 0 < c < CHUNKS:
+        for c in range(CHUNKS):
+            last = c == CHUNKS - 1
+            planes_mu = activate(MU, banks_mu)
+            if not last:
+                banks_mu = layer1(c + 1, MU)
+            if c == 0:
+                quantise_x(2, 0, x_raw[0])
+                log_var_raw = out_tile("biased1")
+                add_b2(SIG, acc_sig, log_var_raw)
+                x_raw.append(copy_x(1, xt))
+                xt = transpose_x(3)
+                quantise_x(2, 1, x_raw[1])
+            if not last:
                 planes_sig = activate(SIG, banks_sig)
-            if c > 0:
-                std = exp_half(log_var)
-            if c < CHUNKS:
-                grouped_sig = interleave_h(SIG, planes_sig)
-                if c + 1 < CHUNKS:
-                    banks_sig = layer1(c + 1, SIG)
-                acc_sig = layer2(SIG, grouped_sig)
-            if c > 0:
-                samples(c - 1, lrelu_biased(MU, acc_mu), std)
             if c + 2 < CHUNKS:
-                xt_next = transpose_x(c + 2)
-            if c < CHUNKS:
-                planes_mu = activate(MU, banks_mu)
-                if c + 1 < CHUNKS:
-                    banks_mu = layer1(c + 1, MU)
-                log_var = clipped(lrelu_biased(SIG, acc_sig))
-                acc_mu = layer2(MU, interleave_h(MU, planes_mu))
-            if c + 2 < CHUNKS:
-                quantise_x(c + 2, xt_next)
+                banks_sig = layer1(c + 2, SIG)
+            h_mu = lrelu_mu(planes_mu)
+            log_var = out_tile("lrelu1")
+            lrelu_out(log_var_raw, log_var)
+            if last:
+                z = scale_noise(c - 1, std)
+            acc_mu = layer2(MU, h_mu)
+            clip(log_var)
+            if c == 0:
+                x_raw = [copy_x(g, xt) for g in range(PASSES1)]
+            if not last:
+                h_sig = interleave_sig(nc.vector.tensor_copy if c == 0 else nc.scalar.copy, planes_sig)
+            if c == 0:
+                for g in range(PASSES1):
+                    quantise_x(3, g, x_raw[g])
+            if 0 < c and not last:
+                z = scale_noise(c - 1, std)
+            std = exp_half(log_var)
+            if last:
+                break
+            mean_raw = out_tile("biased0")
+            add_b2(MU, acc_mu, mean_raw)
+            acc_sig = layer2(SIG, h_sig)
+            if c > 0:
+                add_mean(c - 1, z, mean)
+            mean = out_tile("lrelu0")
+            lrelu_out(mean_raw, mean)
+            log_var_raw = out_tile("biased1")
+            add_b2(SIG, acc_sig, log_var_raw)
+
+        add_mean(CHUNKS - 2, z, mean)
+        z = scale_noise(CHUNKS - 1, std)
+        mean_raw = out_tile("biased0")
+        mean = out_tile("lrelu0")
+        halves = [slice(i, i + 1) for i in range(CHUNK_TILES)]
+        for tiles in halves:
+            add_b2(MU, acc_mu, mean_raw, tiles)
+        for tiles in halves:
+            lrelu_out(mean_raw, mean, tiles)
+        for tiles in halves:
+            add_mean(CHUNKS - 1, z, mean, tiles)

@@ -70,14 +70,6 @@ def tile_infovae_pa_kernel(
         nc.vector.memset(b1_rows[:], 0.0)
         nc.vector.memset(b2_rows[:], 0.0)
         nc.vector.memset(ones[:], 1.0)
-        for r in (MU, SIG):
-            nc.scalar.dma_start(
-                out=b1_rows[H_TILES * r : H_TILES * (r + 1), :], in_=b1[r].rearrange("(m p) -> m p", p=P)
-            )
-            nc.scalar.dma_start(
-                out=b2_rows[0:1, H2 * r : H2 * (r + 1)], in_=b2[r].rearrange("(a o) -> a o", a=1)
-            )
-
         x_sb = keep.tile([P, B_TILES, H0], BF16)
         x_rows = x.rearrange("(p i) k -> p i k", i=B_TILES)
         w1_raw = keep.tile([P, 2, PASSES1, PACK, H1], BF16)
@@ -96,6 +88,13 @@ def tile_infovae_pa_kernel(
         load_w1(SIG, 0)
         load_w1(SIG, 1)
         load_x_pair(0)
+        for r in (MU, SIG):
+            nc.sync.dma_start(
+                out=b1_rows[H_TILES * r : H_TILES * (r + 1), :], in_=b1[r].rearrange("(m p) -> m p", p=P)
+            )
+            nc.sync.dma_start(
+                out=b2_rows[0:1, H2 * r : H2 * (r + 1)], in_=b2[r].rearrange("(a o) -> a o", a=1)
+            )
         load_x_pair(1)
         load_w1(MU, 0)
         load_w1(MU, 1)
@@ -106,13 +105,8 @@ def tile_infovae_pa_kernel(
         nc.sync.dma_start(out=noise[:, 0], in_=noise_enc.rearrange("(p i) o -> p i o", i=B_TILES))
         nc.sync.dma_start(out=noise[:, 1], in_=noise_z.rearrange("(p i) o -> p i o", i=B_TILES))
 
-        bias_ps = psum_o.tile([P, 2 * H2 + 2 * H_TILES], F32, tag="out0")
-        nc.tensor.matmul(bias_ps[:, 2 * H2 :], lhsT=b1_rows[:], rhs=ident_cols[:], start=True, stop=True)
-        nc.tensor.matmul(bias_ps[:, 0 : 2 * H2], lhsT=ones[:], rhs=b2_rows[:], start=True, stop=True)
         b1_col = keep.tile([P, 2 * H_TILES], F32)
-        nc.vector.tensor_copy(out=b1_col[:], in_=bias_ps[:, 2 * H2 :])
         b2_all = keep.tile([P, 2 * H2], F32)
-        nc.vector.tensor_copy(out=b2_all[:], in_=bias_ps[:, 0 : 2 * H2])
 
         w2_grouped = keep.tile([P, 2, H2, PACK], BF16, align_bytes=64)
         w2_codes = keep.tile([P, 2 * H2], U32, align_bytes=64)
@@ -311,9 +305,14 @@ def tile_infovae_pa_kernel(
         for g in range(PASSES1):
             quantise_x(0, g, x_raw[g])
         xt = transpose_x(1)
+        bias_ps = psum_o.tile([P, 2 * H2 + 2 * H_TILES], F32, tag="out0")
+        nc.tensor.matmul(bias_ps[:, 2 * H2 :], lhsT=b1_rows[:], rhs=ident_cols[:], start=True, stop=True)
+        nc.tensor.matmul(bias_ps[:, 0 : 2 * H2], lhsT=ones[:], rhs=b2_rows[:], start=True, stop=True)
+        nc.vector.tensor_copy(out=b1_col[:], in_=bias_ps[:, 2 * H2 :])
         banks_sig = layer1(0, SIG)
         x_raw = [copy_x(g, xt) for g in range(PASSES1)]
         mu_raw = interleave_w1(MU, 0)
+        nc.vector.tensor_copy(out=b2_all[:], in_=bias_ps[:, 0 : 2 * H2])
         planes_sig = activate(SIG, banks_sig)
         quantise_x(1, 0, x_raw[0])
         quantise_w1(MU, 0, mu_raw)

@@ -1,3 +1,4 @@
+import math
 from contextlib import ExitStack
 
 import concourse.mybir as mybir
@@ -18,6 +19,7 @@ K_PASS = P * PACK
 B, H0, H1, H2 = 1024, 1024, 512, 128
 NEG_SLOPE = 0.01
 LV_MIN, LV_MAX = -10.0, 10.0
+STD_MIN, STD_MAX = math.exp(0.5 * LV_MIN), math.exp(0.5 * LV_MAX)
 
 B_TILES = B // P
 PAIRS = B_TILES // 2
@@ -27,7 +29,8 @@ H_TILES = H1 // P
 CHUNKS = PAIRS
 CHUNK_TILES = B_TILES // CHUNKS
 CHUNK_COLS = CHUNK_TILES * P
-W1_VECTOR_COLS = 384
+BIASES = 2 * H_TILES + 2
+W1_VECTOR_COLS = 352
 
 MU, SIG = 0, 1
 
@@ -59,17 +62,11 @@ def tile_infovae_pa_kernel(
 
         ident = keep.tile([P, P], F32)
         make_identity(nc, ident[:])
-        ident_cols = keep.tile([P, 2 * H_TILES], BF16)
-        nc.gpsimd.tensor_copy(out=ident_cols[:], in_=ident[:, 0 : 2 * H_TILES])
+        ident_cols = keep.tile([P, BIASES], BF16)
+        nc.gpsimd.tensor_copy(out=ident_cols[:], in_=ident[:, 0:BIASES])
 
-        ctx.enter_context(tc.manual_schedule())
-
-        b1_rows = keep.tile([P, P], BF16)
-        b2_rows = keep.tile([P, 2 * H2], BF16)
-        ones = keep.tile([P, P], BF16)
-        nc.vector.memset(b1_rows[:], 0.0)
-        nc.vector.memset(b2_rows[:], 0.0)
-        nc.vector.memset(ones[:], 1.0)
+        bias_rows = keep.tile([P, P], BF16)
+        nc.vector.memset(bias_rows[:], 0.0)
         x_sb = keep.tile([P, B_TILES, H0], BF16)
         x_rows = x.rearrange("(p i) k -> p i k", i=B_TILES)
         w1_raw = keep.tile([P, 2, PASSES1, PACK, H1], BF16)
@@ -90,10 +87,10 @@ def tile_infovae_pa_kernel(
         load_x_pair(0)
         for r in (MU, SIG):
             nc.sync.dma_start(
-                out=b1_rows[H_TILES * r : H_TILES * (r + 1), :], in_=b1[r].rearrange("(m p) -> m p", p=P)
+                out=bias_rows[H_TILES * r : H_TILES * (r + 1), :], in_=b1[r].rearrange("(m p) -> m p", p=P)
             )
             nc.sync.dma_start(
-                out=b2_rows[0:1, H2 * r : H2 * (r + 1)], in_=b2[r].rearrange("(a o) -> a o", a=1)
+                out=bias_rows[2 * H_TILES + r : 2 * H_TILES + r + 1, :], in_=b2[r].rearrange("(a o) -> a o", a=1)
             )
         load_x_pair(1)
         load_w1(MU, 0)
@@ -105,8 +102,22 @@ def tile_infovae_pa_kernel(
         nc.sync.dma_start(out=noise[:, 0], in_=noise_enc.rearrange("(p i) o -> p i o", i=B_TILES))
         nc.sync.dma_start(out=noise[:, 1], in_=noise_z.rearrange("(p i) o -> p i o", i=B_TILES))
 
-        b1_col = keep.tile([P, 2 * H_TILES], F32)
-        b2_all = keep.tile([P, 2 * H2], F32)
+        bias_col = keep.tile([P, BIASES], F32)
+        half_b2_sig = keep.tile([P, 2], F32)
+
+        def transpose_biases():
+            bias_ps = psum_o.tile([P, BIASES], F32, tag="out0")
+            nc.tensor.matmul(bias_ps[:], lhsT=bias_rows[:], rhs=ident_cols[:], start=True, stop=True)
+            nc.vector.tensor_copy(out=bias_col[:], in_=bias_ps[:])
+            for e, slope in enumerate((1.0, NEG_SLOPE)):
+                nc.gpsimd.tensor_scalar(
+                    out=half_b2_sig[:, e : e + 1],
+                    in0=bias_col[:, BIASES - 1 : BIASES],
+                    scalar1=0.5 * slope,
+                    scalar2=0.0,
+                    op0=ALU.mult,
+                    op1=ALU.add,
+                )
 
         w2_grouped = keep.tile([P, 2, H2, PACK], BF16, align_bytes=64)
         w2_codes = keep.tile([P, 2 * H2], U32, align_bytes=64)
@@ -195,7 +206,7 @@ def tile_infovae_pa_kernel(
                     out=planes[:, m, :],
                     in_=banks[m // 2][:, m % 2, :],
                     func=ACT.Tanh if r == SIG else ACT.Identity,
-                    bias=b1_col[:, H_TILES * r + m : H_TILES * r + m + 1],
+                    bias=bias_col[:, H_TILES * r + m : H_TILES * r + m + 1],
                     scale=1.0,
                 )
             return planes
@@ -205,96 +216,94 @@ def tile_infovae_pa_kernel(
             interleave_rows(copy, h_grouped[:], planes[:])
             return h_grouped
 
-        def lrelu_mu(planes):
-            h_grouped = stage.tile([P, CHUNK_COLS, PACK], BF16, align_bytes=64, tag="h_grouped0")
-            by_column = planes[:].rearrange("p m b -> p b m")
+        def lrelu_mu(planes, n=CHUNK_COLS, first=0):
+            h_grouped = stage.tile([P, n, PACK], BF16, align_bytes=64, tag="h_grouped0")
+            by_column = planes[:, :, first : first + n].rearrange("p m b -> p b m")
             nc.vector.scalar_tensor_tensor(
                 out=h_grouped[:], in0=by_column, scalar=NEG_SLOPE, in1=by_column, op0=ALU.mult, op1=ALU.max
             )
             return h_grouped
 
-        def layer2(r, h_grouped):
-            h_codes = stage.tile([P, CHUNK_COLS], U32, align_bytes=64, tag="h_codes%d" % r)
-            h_scales = stage.tile([P, CHUNK_COLS], U8, align_bytes=64, tag="h_scales%d" % r)
+        def layer2(r, h_grouped, n=CHUNK_COLS, bank=None):
+            h_codes = stage.tile([P, n], U32, align_bytes=64, tag="h_codes%d" % r)
+            h_scales = stage.tile([P, n], U8, align_bytes=64, tag="h_scales%d" % r)
             nc.vector.quantize_mx(
                 out=h_codes[:].bitcast(FP8X4), scales=h_scales[:], in_=h_grouped[:].rearrange("p b m -> p (b m)")
             )
             outs = slice(H2 * r, H2 * (r + 1))
-            acc = psum_o.tile([P, CHUNK_TILES, H2], F32, tag="out%d" % r)
-            for i in range(CHUNK_TILES):
-                rows = slice(P * i, P * (i + 1))
-                nc.tensor.matmul_mx(
-                    out=acc[:, i, :],
-                    lhsT=h_codes[:, rows].bitcast(FP8X4),
-                    lhsT_scale=h_scales[:, rows],
-                    rhs=w2_codes[:, outs].bitcast(FP8X4),
-                    rhs_scale=w2_scales[:, outs],
-                    start=True,
-                    stop=True,
-                )
+            acc = psum_o.tile([P, n], F32, tag="out%d" % (r if bank is None else bank))
+            nc.tensor.matmul_mx(
+                out=acc[:],
+                lhsT=w2_codes[:, outs].bitcast(FP8X4),
+                lhsT_scale=w2_scales[:, outs],
+                rhs=h_codes[:].bitcast(FP8X4),
+                rhs_scale=h_scales[:],
+                start=True,
+                stop=True,
+            )
             return acc
 
-        whole = slice(0, CHUNK_TILES)
+        def exponentials(acc):
+            exps = stage.tile([P, 2, CHUNK_COLS], F32, tag="exps")
+            for e, slope in enumerate((1.0, NEG_SLOPE)):
+                nc.scalar.activation(
+                    out=exps[:, e, :], in_=acc[:], func=ACT.Exp, bias=half_b2_sig[:, e : e + 1], scale=0.5 * slope
+                )
+            return exps
 
-        def add_b2(r, acc, biased, tiles=whole):
-            shape = [P, tiles.stop - tiles.start, H2]
-            nc.vector.tensor_tensor(
-                out=biased[:, tiles, :],
-                in0=acc[:, tiles, :],
-                in1=b2_all[:, H2 * r : H2 * (r + 1)].unsqueeze(1).to_broadcast(shape),
-                op=ALU.add,
-            )
+        def transpose_back(rows, tiles=CHUNK_TILES):
+            turned = psum_t.tile([P, tiles, H2], F32, tag="xt", name="turned")
+            for i in range(tiles):
+                nc.tensor.transpose(turned[:, i, :], rows[:, P * i : P * (i + 1)], ident[:])
+            return turned
 
-        def lrelu_out(biased, result, tiles=whole):
+        def std_of(exps):
+            std = stage.tile([P, CHUNK_COLS], F32, tag="std")
             nc.vector.scalar_tensor_tensor(
-                out=result[:, tiles, :],
-                in0=biased[:, tiles, :],
-                scalar=NEG_SLOPE,
-                in1=biased[:, tiles, :],
-                op0=ALU.mult,
-                op1=ALU.max,
+                out=std[:], in0=exps[:, 0, :], scalar=STD_MIN, in1=exps[:, 1, :], op0=ALU.max, op1=ALU.max
             )
+            return transpose_back(std)
 
-        def out_tile(name):
-            return stage.tile([P, CHUNK_TILES, H2], F32, tag=name, name=name)
-
-        def clip(log_var):
-            nc.vector.tensor_scalar(
-                out=log_var[:], in0=log_var[:], scalar1=LV_MAX, scalar2=LV_MIN, op0=ALU.min, op1=ALU.max
+        def biased_mean(acc, n=CHUNK_COLS):
+            biased = stage.tile([P, n], F32, tag="biased")
+            nc.scalar.activation(
+                out=biased[:], in_=acc[:], func=ACT.Identity, bias=bias_col[:, BIASES - 2 : BIASES - 1], scale=1.0
             )
+            return biased
 
-        def exp_half(log_var):
-            std = out_tile("std")
-            nc.scalar.activation(out=std[:], in_=log_var[:], func=ACT.Exp, scale=0.5)
-            return std
+        def mean_of(biased, n=CHUNK_COLS):
+            mean = stage.tile([P, n], F32, tag="mean")
+            nc.vector.scalar_tensor_tensor(
+                out=mean[:], in0=biased[:], scalar=NEG_SLOPE, in1=biased[:], op0=ALU.mult, op1=ALU.max
+            )
+            return transpose_back(mean, n // P)
 
         out_rows = (
             out_0.rearrange("(p i) o -> p i o", i=B_TILES),
             out_1.rearrange("(p i) o -> p i o", i=B_TILES),
         )
+        both = [P, 2, CHUNK_TILES, H2]
 
         def scale_noise(c, std):
-            both = [P, 2, CHUNK_TILES, H2]
             z = stage.tile(both, F32, tag="z")
-            nc.vector.tensor_tensor(
+            nc.vector.scalar_tensor_tensor(
                 out=z[:],
-                in0=noise[:, :, CHUNK_TILES * c : CHUNK_TILES * (c + 1), :],
-                in1=std[:].unsqueeze(1).to_broadcast(both),
-                op=ALU.mult,
+                in0=std[:].unsqueeze(1).to_broadcast(both),
+                scalar=STD_MAX,
+                in1=noise[:, :, CHUNK_TILES * c : CHUNK_TILES * (c + 1), :],
+                op0=ALU.min,
+                op1=ALU.mult,
             )
             return z
 
-        def add_mean(c, z, mean, tiles=whole):
-            n_tiles = tiles.stop - tiles.start
+        def add_mean(c, z, mean, first=0, tiles=CHUNK_TILES):
+            part = z[:, :, first : first + tiles, :]
             nc.vector.tensor_tensor(
-                out=z[:, :, tiles, :],
-                in0=z[:, :, tiles, :],
-                in1=mean[:, tiles, :].unsqueeze(1).to_broadcast([P, 2, n_tiles, H2]),
-                op=ALU.add,
+                out=part, in0=part, in1=mean[:].unsqueeze(1).to_broadcast([P, 2, tiles, H2]), op=ALU.add
             )
-            first = CHUNK_TILES * c + tiles.start
+            row = CHUNK_TILES * c + first
             for n in range(2):
-                nc.sync.dma_start(out=out_rows[n][:, first : first + n_tiles, :], in_=z[:, n, tiles, :])
+                nc.sync.dma_start(out=out_rows[n][:, row : row + tiles, :], in_=part[:, n])
 
         sig_raw = [interleave_w1(SIG, 0)]
         xt = transpose_x(0)
@@ -305,14 +314,10 @@ def tile_infovae_pa_kernel(
         for g in range(PASSES1):
             quantise_x(0, g, x_raw[g])
         xt = transpose_x(1)
-        bias_ps = psum_o.tile([P, 2 * H2 + 2 * H_TILES], F32, tag="out0")
-        nc.tensor.matmul(bias_ps[:, 2 * H2 :], lhsT=b1_rows[:], rhs=ident_cols[:], start=True, stop=True)
-        nc.tensor.matmul(bias_ps[:, 0 : 2 * H2], lhsT=ones[:], rhs=b2_rows[:], start=True, stop=True)
-        nc.vector.tensor_copy(out=b1_col[:], in_=bias_ps[:, 2 * H2 :])
+        transpose_biases()
         banks_sig = layer1(0, SIG)
         x_raw = [copy_x(g, xt) for g in range(PASSES1)]
         mu_raw = interleave_w1(MU, 0)
-        nc.vector.tensor_copy(out=b2_all[:], in_=bias_ps[:, 0 : 2 * H2])
         planes_sig = activate(SIG, banks_sig)
         quantise_x(1, 0, x_raw[0])
         quantise_w1(MU, 0, mu_raw)
@@ -330,58 +335,44 @@ def tile_infovae_pa_kernel(
         x_raw = [copy_x(0, xt)]
 
         for c in range(CHUNKS):
-            last = c == CHUNKS - 1
             planes_mu = activate(MU, banks_mu)
-            if not last:
-                banks_mu = layer1(c + 1, MU)
+            if c + 1 == CHUNKS:
+                break
+            banks_mu = layer1(c + 1, MU)
             if c == 0:
                 quantise_x(2, 0, x_raw[0])
-                log_var_raw = out_tile("biased1")
-                add_b2(SIG, acc_sig, log_var_raw)
                 x_raw.append(copy_x(1, xt))
                 xt = transpose_x(3)
                 quantise_x(2, 1, x_raw[1])
-            if not last:
-                planes_sig = activate(SIG, banks_sig)
+            planes_sig = activate(SIG, banks_sig)
+            exps = exponentials(acc_sig)
+            h_mu = lrelu_mu(planes_mu)
+            if c > 0:
+                add_mean(c - 1, z, mean)
+            acc_mu = layer2(MU, h_mu)
+            std = std_of(exps)
             if c + 2 < CHUNKS:
                 banks_sig = layer1(c + 2, SIG)
-            h_mu = lrelu_mu(planes_mu)
-            log_var = out_tile("lrelu1")
-            lrelu_out(log_var_raw, log_var)
-            if last:
-                z = scale_noise(c - 1, std)
-            acc_mu = layer2(MU, h_mu)
-            clip(log_var)
             if c == 0:
                 x_raw = [copy_x(g, xt) for g in range(PASSES1)]
-            if not last:
-                h_sig = interleave_sig(nc.vector.tensor_copy if c == 0 else nc.scalar.copy, planes_sig)
+            h_sig = interleave_sig(nc.vector.tensor_copy, planes_sig)
             if c == 0:
                 for g in range(PASSES1):
                     quantise_x(3, g, x_raw[g])
-            if 0 < c and not last:
-                z = scale_noise(c - 1, std)
-            std = exp_half(log_var)
-            if last:
-                break
-            mean_raw = out_tile("biased0")
-            add_b2(MU, acc_mu, mean_raw)
+            biased = biased_mean(acc_mu)
             acc_sig = layer2(SIG, h_sig)
-            if c > 0:
-                add_mean(c - 1, z, mean)
-            mean = out_tile("lrelu0")
-            lrelu_out(mean_raw, mean)
-            log_var_raw = out_tile("biased1")
-            add_b2(SIG, acc_sig, log_var_raw)
+            z = scale_noise(c, std)
+            mean = mean_of(biased)
 
+        exps = exponentials(acc_sig)
+        tiles = range(CHUNK_TILES)
+        h_mu = [lrelu_mu(planes_mu, P, P * i) for i in tiles]
+        acc_mu = [layer2(MU, h_mu[0], P)]
         add_mean(CHUNKS - 2, z, mean)
+        acc_mu.append(layer2(MU, h_mu[1], P, SIG))
+        std = std_of(exps)
+        biased = [biased_mean(acc_mu[i], P) for i in tiles]
         z = scale_noise(CHUNKS - 1, std)
-        mean_raw = out_tile("biased0")
-        mean = out_tile("lrelu0")
-        halves = [slice(i, i + 1) for i in range(CHUNK_TILES)]
-        for tiles in halves:
-            add_b2(MU, acc_mu, mean_raw, tiles)
-        for tiles in halves:
-            lrelu_out(mean_raw, mean, tiles)
-        for tiles in halves:
-            add_mean(CHUNKS - 1, z, mean, tiles)
+        mean = [mean_of(biased[i], P) for i in tiles]
+        for i in tiles:
+            add_mean(CHUNKS - 1, z, mean[i], i, 1)

@@ -30,7 +30,7 @@ CHUNKS = PAIRS
 CHUNK_TILES = B_TILES // CHUNKS
 CHUNK_COLS = CHUNK_TILES * P
 BIASES = 2 * H_TILES + 2
-W1_VECTOR_COLS = 352
+W1_VECTOR_COLS = 320
 
 MU, SIG = 0, 1
 
@@ -83,8 +83,8 @@ def tile_infovae_pa_kernel(
             )
 
         load_w1(SIG, 0)
-        load_w1(SIG, 1)
         load_x_pair(0)
+        load_w1(SIG, 1)
         for r in (MU, SIG):
             nc.sync.dma_start(
                 out=bias_rows[H_TILES * r : H_TILES * (r + 1), :], in_=b1[r].rearrange("(m p) -> m p", p=P)
@@ -133,8 +133,8 @@ def tile_infovae_pa_kernel(
                 in_=w2_grouped[:].rearrange("p r o m -> p (r o m)"),
             )
 
-        x_codes = keep.tile([P, PASSES1, B], U32, align_bytes=64)
-        x_scales = keep.tile([P, PASSES1, B], U8, align_bytes=64)
+        x_codes = keep.tile([P, PAIRS, PASSES1, PAIR_COLS], U32, align_bytes=64)
+        x_scales = keep.tile([P, PAIRS, PASSES1, PAIR_COLS], U8, align_bytes=64)
         w1_codes = keep.tile([P, 2, PASSES1, H1], U32, align_bytes=64)
         w1_scales = keep.tile([P, 2, PASSES1, H1], U8, align_bytes=64)
 
@@ -166,22 +166,21 @@ def tile_infovae_pa_kernel(
                 banks.append(xt)
             return banks
 
-        def copy_x(g, banks):
-            x_grouped = stage.tile([P, PAIR_COLS * PACK], BF16, align_bytes=64, tag="x_grouped")
-            nc.scalar.copy(
-                out=x_grouped[:].bitcast(F32).rearrange("p (b u) -> p b u", u=2),
-                in_=banks[g][:].rearrange("p u b -> p b u"),
-            )
+        def copy_x(banks):
+            x_grouped = stage.tile([P, PASSES1 * PAIR_COLS * PACK], BF16, align_bytes=64, tag="x_grouped")
+            words = x_grouped[:].bitcast(F32).rearrange("p (g b u) -> p g b u", g=PASSES1, u=2)
+            for g in range(PASSES1):
+                nc.scalar.copy(out=words[:, g], in_=banks[g][:].rearrange("p u b -> p b u"))
             return x_grouped
 
-        def quantise_x(j, g, x_grouped):
-            cols = slice(PAIR_COLS * j, PAIR_COLS * (j + 1))
+        def quantise_x(j, x_grouped):
             nc.vector.quantize_mx(
-                out=x_codes[:, g, cols].bitcast(FP8X4), scales=x_scales[:, g, cols], in_=x_grouped[:]
+                out=x_codes[:, j].rearrange("p g b -> p (g b)").bitcast(FP8X4),
+                scales=x_scales[:, j].rearrange("p g b -> p (g b)"),
+                in_=x_grouped[:],
             )
 
         def layer1(c, r):
-            cols = slice(CHUNK_COLS * c, CHUNK_COLS * (c + 1))
             banks = []
             for m in range(H_TILES):
                 units = slice(P * m, P * (m + 1))
@@ -192,8 +191,8 @@ def tile_infovae_pa_kernel(
                         out=banks[m // 2][:, m % 2, :],
                         lhsT=w1_codes[:, r, g, units].bitcast(FP8X4),
                         lhsT_scale=w1_scales[:, r, g, units],
-                        rhs=x_codes[:, g, cols].bitcast(FP8X4),
-                        rhs_scale=x_scales[:, g, cols],
+                        rhs=x_codes[:, c, g, :].bitcast(FP8X4),
+                        rhs_scale=x_scales[:, c, g, :],
                         start=(g == 0),
                         stop=(g == PASSES1 - 1),
                     )
@@ -305,34 +304,33 @@ def tile_infovae_pa_kernel(
             for n in range(2):
                 nc.sync.dma_start(out=out_rows[n][:, row : row + tiles, :], in_=part[:, n])
 
-        sig_raw = [interleave_w1(SIG, 0)]
-        xt = transpose_x(0)
-        sig_raw.append(interleave_w1(SIG, 1))
-        quantise_w1(SIG, 0, sig_raw[0])
-        x_raw = [copy_x(g, xt) for g in range(PASSES1)]
-        quantise_w1(SIG, 1, sig_raw[1])
-        for g in range(PASSES1):
-            quantise_x(0, g, x_raw[g])
-        xt = transpose_x(1)
-        transpose_biases()
-        banks_sig = layer1(0, SIG)
-        x_raw = [copy_x(g, xt) for g in range(PASSES1)]
-        mu_raw = interleave_w1(MU, 0)
-        planes_sig = activate(SIG, banks_sig)
-        quantise_x(1, 0, x_raw[0])
-        quantise_w1(MU, 0, mu_raw)
-        quantise_x(1, 1, x_raw[1])
-        banks_sig = layer1(1, SIG)
-        xt = transpose_x(2)
-        mu_raw = interleave_w1(MU, 1)
-        interleave_w2(SIG)
-        quantise_w1(MU, 1, mu_raw)
-        interleave_w2(MU)
-        h_sig = interleave_sig(nc.vector.tensor_copy, planes_sig)
-        quantise_w2()
-        banks_mu = layer1(0, MU)
-        acc_sig = layer2(SIG, h_sig)
-        x_raw = [copy_x(0, xt)]
+        with tc.manual_schedule():
+            sig_grouped_0 = interleave_w1(SIG, 0)
+            xt = transpose_x(0)
+            quantise_w1(SIG, 0, sig_grouped_0)
+            x_raw = copy_x(xt)
+            sig_grouped_1 = interleave_w1(SIG, 1)
+            quantise_x(0, x_raw)
+            quantise_w1(SIG, 1, sig_grouped_1)
+            xt = transpose_x(1)
+            transpose_biases()
+            banks_sig = layer1(0, SIG)
+            x_raw = copy_x(xt)
+            mu_grouped_0 = interleave_w1(MU, 0)
+            quantise_x(1, x_raw)
+            planes_sig = activate(SIG, banks_sig)
+            mu_grouped_1 = interleave_w1(MU, 1)
+            quantise_w1(MU, 0, mu_grouped_0)
+            banks_sig = layer1(1, SIG)
+            xt = transpose_x(2)
+            interleave_w2(SIG)
+            interleave_w2(MU)
+            quantise_w1(MU, 1, mu_grouped_1)
+            h_sig = interleave_sig(nc.vector.tensor_copy, planes_sig)
+            quantise_w2()
+            banks_mu = layer1(0, MU)
+            acc_sig = layer2(SIG, h_sig)
+        x_raw = copy_x(xt)
 
         for c in range(CHUNKS):
             planes_mu = activate(MU, banks_mu)
@@ -340,10 +338,8 @@ def tile_infovae_pa_kernel(
                 break
             banks_mu = layer1(c + 1, MU)
             if c == 0:
-                quantise_x(2, 0, x_raw[0])
-                x_raw.append(copy_x(1, xt))
+                quantise_x(2, x_raw)
                 xt = transpose_x(3)
-                quantise_x(2, 1, x_raw[1])
             planes_sig = activate(SIG, banks_sig)
             exps = exponentials(acc_sig)
             h_mu = lrelu_mu(planes_mu)
@@ -354,24 +350,27 @@ def tile_infovae_pa_kernel(
             if c + 2 < CHUNKS:
                 banks_sig = layer1(c + 2, SIG)
             if c == 0:
-                x_raw = [copy_x(g, xt) for g in range(PASSES1)]
-            h_sig = interleave_sig(nc.vector.tensor_copy, planes_sig)
+                x_raw = copy_x(xt)
+            if c + 2 < CHUNKS:
+                h_sig = interleave_sig(nc.vector.tensor_copy, planes_sig)
             if c == 0:
-                for g in range(PASSES1):
-                    quantise_x(3, g, x_raw[g])
+                quantise_x(3, x_raw)
             biased = biased_mean(acc_mu)
-            acc_sig = layer2(SIG, h_sig)
+            if c + 2 < CHUNKS:
+                acc_sig = layer2(SIG, h_sig)
             z = scale_noise(c, std)
             mean = mean_of(biased)
 
-        exps = exponentials(acc_sig)
+        h_sig = interleave_sig(nc.scalar.copy, planes_sig)
         tiles = range(CHUNK_TILES)
         h_mu = [lrelu_mu(planes_mu, P, P * i) for i in tiles]
         acc_mu = [layer2(MU, h_mu[0], P)]
+        acc_sig = layer2(SIG, h_sig)
         add_mean(CHUNKS - 2, z, mean)
+        exps = exponentials(acc_sig)
         acc_mu.append(layer2(MU, h_mu[1], P, SIG))
-        std = std_of(exps)
         biased = [biased_mean(acc_mu[i], P) for i in tiles]
+        std = std_of(exps)
         z = scale_noise(CHUNKS - 1, std)
         mean = [mean_of(biased[i], P) for i in tiles]
         for i in tiles:

@@ -138,8 +138,10 @@ def tile_infovae_pa_kernel(
         w1_codes = keep.tile([P, 2, PASSES1, H1], U32, align_bytes=64)
         w1_scales = keep.tile([P, 2, PASSES1, H1], U8, align_bytes=64)
 
-        def interleave_w1(r, g):
-            w1_grouped = stage.tile([P, H1, PACK], BF16, align_bytes=64, tag="w1_grouped")
+        def w1_tile():
+            return stage.tile([P, H1, PACK], BF16, align_bytes=64, tag="w1_grouped", name="w1_grouped")
+
+        def interleave_w1(r, g, w1_grouped):
             v = W1_VECTOR_COLS
             interleave_rows(nc.vector.tensor_copy, w1_grouped[:, :v, :], w1_raw[:, r, g, :, :v])
             interleave_rows(nc.scalar.copy, w1_grouped[:, v:, :], w1_raw[:, r, g, :, v:])
@@ -166,11 +168,17 @@ def tile_infovae_pa_kernel(
                 banks.append(xt)
             return banks
 
-        def copy_x(banks):
+        def x_tile():
             x_grouped = stage.tile([P, PASSES1 * PAIR_COLS * PACK], BF16, align_bytes=64, tag="x_grouped")
-            words = x_grouped[:].bitcast(F32).rearrange("p (g b u) -> p g b u", g=PASSES1, u=2)
+            return x_grouped, x_grouped[:].bitcast(F32).rearrange("p (g b u) -> p g b u", g=PASSES1, u=2)
+
+        def by_column(bank):
+            return bank[:].rearrange("p u b -> p b u")
+
+        def copy_x(banks):
+            x_grouped, words = x_tile()
             for g in range(PASSES1):
-                nc.scalar.copy(out=words[:, g], in_=banks[g][:].rearrange("p u b -> p b u"))
+                nc.scalar.copy(out=words[:, g], in_=by_column(banks[g]))
             return x_grouped
 
         def quantise_x(j, x_grouped):
@@ -217,20 +225,24 @@ def tile_infovae_pa_kernel(
 
         def lrelu_mu(planes, n=CHUNK_COLS, first=0):
             h_grouped = stage.tile([P, n, PACK], BF16, align_bytes=64, tag="h_grouped0")
-            by_column = planes[:, :, first : first + n].rearrange("p m b -> p b m")
+            columns = planes[:, :, first : first + n].rearrange("p m b -> p b m")
             nc.vector.scalar_tensor_tensor(
-                out=h_grouped[:], in0=by_column, scalar=NEG_SLOPE, in1=by_column, op0=ALU.mult, op1=ALU.max
+                out=h_grouped[:], in0=columns, scalar=NEG_SLOPE, in1=columns, op0=ALU.mult, op1=ALU.max
             )
             return h_grouped
 
-        def layer2(r, h_grouped, n=CHUNK_COLS, bank=None):
+        def quantise_h(r, h_grouped, n):
             h_codes = stage.tile([P, n], U32, align_bytes=64, tag="h_codes%d" % r)
             h_scales = stage.tile([P, n], U8, align_bytes=64, tag="h_scales%d" % r)
             nc.vector.quantize_mx(
                 out=h_codes[:].bitcast(FP8X4), scales=h_scales[:], in_=h_grouped[:].rearrange("p b m -> p (b m)")
             )
+            return h_codes, h_scales
+
+        def layer2(r, h_grouped):
+            h_codes, h_scales = quantise_h(r, h_grouped, CHUNK_COLS)
             outs = slice(H2 * r, H2 * (r + 1))
-            acc = psum_o.tile([P, n], F32, tag="out%d" % (r if bank is None else bank))
+            acc = psum_o.tile([P, CHUNK_COLS], F32, tag="out%d" % r)
             nc.tensor.matmul_mx(
                 out=acc[:],
                 lhsT=w2_codes[:, outs].bitcast(FP8X4),
@@ -242,6 +254,33 @@ def tile_infovae_pa_kernel(
             )
             return acc
 
+        def layer2_mu_rows(h_grouped, bank):
+            h_codes, h_scales = quantise_h(MU, h_grouped, P)
+            acc = psum_o.tile([P, H2], F32, tag="out%d" % bank)
+            nc.tensor.matmul_mx(
+                out=acc[:],
+                lhsT=h_codes[:].bitcast(FP8X4),
+                lhsT_scale=h_scales[:],
+                rhs=w2_codes[:, 0:H2].bitcast(FP8X4),
+                rhs_scale=w2_scales[:, 0:H2],
+                start=True,
+                stop=True,
+            )
+            return acc
+
+        b2_mu_rows = keep.tile([P, H2], F32)
+
+        def spread_b2_mu():
+            spread = psum_t.tile([P, H2], F32, tag="xt", name="spread")
+            nc.tensor.matmul(
+                spread[:],
+                lhsT=bias_col[:, BIASES - 2 : BIASES - 1].to_broadcast([P, P]),
+                rhs=ident[:],
+                start=True,
+                stop=True,
+            )
+            nc.scalar.copy(out=b2_mu_rows[:], in_=spread[:])
+
         def exponentials(acc):
             exps = stage.tile([P, 2, CHUNK_COLS], F32, tag="exps")
             for e, slope in enumerate((1.0, NEG_SLOPE)):
@@ -250,9 +289,9 @@ def tile_infovae_pa_kernel(
                 )
             return exps
 
-        def transpose_back(rows, tiles=CHUNK_TILES):
-            turned = psum_t.tile([P, tiles, H2], F32, tag="xt", name="turned")
-            for i in range(tiles):
+        def transpose_back(rows):
+            turned = psum_t.tile([P, CHUNK_TILES, H2], F32, tag="xt", name="turned")
+            for i in range(CHUNK_TILES):
                 nc.tensor.transpose(turned[:, i, :], rows[:, P * i : P * (i + 1)], ident[:])
             return turned
 
@@ -263,19 +302,27 @@ def tile_infovae_pa_kernel(
             )
             return transpose_back(std)
 
-        def biased_mean(acc, n=CHUNK_COLS):
-            biased = stage.tile([P, n], F32, tag="biased")
+        def biased_mean(acc):
+            biased = stage.tile([P, CHUNK_COLS], F32, tag="biased")
             nc.scalar.activation(
                 out=biased[:], in_=acc[:], func=ACT.Identity, bias=bias_col[:, BIASES - 2 : BIASES - 1], scale=1.0
             )
             return biased
 
-        def mean_of(biased, n=CHUNK_COLS):
+        def lrelu_mean(biased, n):
             mean = stage.tile([P, n], F32, tag="mean")
             nc.vector.scalar_tensor_tensor(
                 out=mean[:], in0=biased[:], scalar=NEG_SLOPE, in1=biased[:], op0=ALU.mult, op1=ALU.max
             )
-            return transpose_back(mean, n // P)
+            return mean
+
+        def mean_of(biased):
+            return transpose_back(lrelu_mean(biased, CHUNK_COLS))
+
+        def biased_rows(acc):
+            biased = stage.tile([P, H2], F32, tag="biased")
+            nc.vector.tensor_tensor(out=biased[:], in0=acc[:], in1=b2_mu_rows[:], op=ALU.add)
+            return biased
 
         out_rows = (
             out_0.rearrange("(p i) o -> p i o", i=B_TILES),
@@ -298,28 +345,35 @@ def tile_infovae_pa_kernel(
         def add_mean(c, z, mean, first=0, tiles=CHUNK_TILES):
             part = z[:, :, first : first + tiles, :]
             nc.vector.tensor_tensor(
-                out=part, in0=part, in1=mean[:].unsqueeze(1).to_broadcast([P, 2, tiles, H2]), op=ALU.add
+                out=part, in0=part, in1=mean.unsqueeze(1).to_broadcast([P, 2, tiles, H2]), op=ALU.add
             )
             row = CHUNK_TILES * c + first
             for n in range(2):
                 nc.sync.dma_start(out=out_rows[n][:, row : row + tiles, :], in_=part[:, n])
 
+        def copy_x_and_interleave(xt):
+            x_grouped, words = x_tile()
+            grouped = w1_tile()
+            nc.scalar.copy(out=words[:, 0], in_=by_column(xt[0]))
+            interleave_w1(SIG, 1, grouped)
+            nc.vector.tensor_copy(out=words[:, 1], in_=by_column(xt[1]))
+            return x_grouped, grouped
+
         with tc.manual_schedule():
-            sig_grouped_0 = interleave_w1(SIG, 0)
+            sig_grouped_0 = interleave_w1(SIG, 0, w1_tile())
             xt = transpose_x(0)
             quantise_w1(SIG, 0, sig_grouped_0)
-            x_raw = copy_x(xt)
-            sig_grouped_1 = interleave_w1(SIG, 1)
+            x_raw, sig_grouped_1 = copy_x_and_interleave(xt)
             quantise_x(0, x_raw)
             quantise_w1(SIG, 1, sig_grouped_1)
             xt = transpose_x(1)
             transpose_biases()
             banks_sig = layer1(0, SIG)
             x_raw = copy_x(xt)
-            mu_grouped_0 = interleave_w1(MU, 0)
+            mu_grouped_0 = interleave_w1(MU, 0, w1_tile())
             quantise_x(1, x_raw)
             planes_sig = activate(SIG, banks_sig)
-            mu_grouped_1 = interleave_w1(MU, 1)
+            mu_grouped_1 = interleave_w1(MU, 1, w1_tile())
             quantise_w1(MU, 0, mu_grouped_0)
             banks_sig = layer1(1, SIG)
             xt = transpose_x(2)
@@ -331,6 +385,7 @@ def tile_infovae_pa_kernel(
             banks_mu = layer1(0, MU)
             acc_sig = layer2(SIG, h_sig)
         x_raw = copy_x(xt)
+        spread_b2_mu()
 
         for c in range(CHUNKS):
             planes_mu = activate(MU, banks_mu)
@@ -344,7 +399,7 @@ def tile_infovae_pa_kernel(
             exps = exponentials(acc_sig)
             h_mu = lrelu_mu(planes_mu)
             if c > 0:
-                add_mean(c - 1, z, mean)
+                add_mean(c - 1, z, mean[:])
             acc_mu = layer2(MU, h_mu)
             std = std_of(exps)
             if c + 2 < CHUNKS:
@@ -363,15 +418,16 @@ def tile_infovae_pa_kernel(
 
         h_sig = interleave_sig(nc.scalar.copy, planes_sig)
         tiles = range(CHUNK_TILES)
-        h_mu = [lrelu_mu(planes_mu, P, P * i) for i in tiles]
-        acc_mu = [layer2(MU, h_mu[0], P)]
         acc_sig = layer2(SIG, h_sig)
-        add_mean(CHUNKS - 2, z, mean)
+        h_mu = [lrelu_mu(planes_mu, P, 0)]
         exps = exponentials(acc_sig)
-        acc_mu.append(layer2(MU, h_mu[1], P, SIG))
-        biased = [biased_mean(acc_mu[i], P) for i in tiles]
+        acc_mu = [layer2_mu_rows(h_mu[0], MU)]
         std = std_of(exps)
+        h_mu.append(lrelu_mu(planes_mu, P, P))
+        add_mean(CHUNKS - 2, z, mean[:])
+        acc_mu.append(layer2_mu_rows(h_mu[1], SIG))
         z = scale_noise(CHUNKS - 1, std)
-        mean = [mean_of(biased[i], P) for i in tiles]
+        biased = [biased_rows(acc_mu[i]) for i in tiles]
+        mean = [lrelu_mean(biased[i], P) for i in tiles]
         for i in tiles:
-            add_mean(CHUNKS - 1, z, mean[i], i, 1)
+            add_mean(CHUNKS - 1, z, mean[i][:].unsqueeze(1), i, 1)

@@ -138,10 +138,8 @@ def tile_infovae_pa_kernel(
         w1_codes = keep.tile([P, 2, PASSES1, H1], U32, align_bytes=64)
         w1_scales = keep.tile([P, 2, PASSES1, H1], U8, align_bytes=64)
 
-        def w1_tile():
-            return stage.tile([P, H1, PACK], BF16, align_bytes=64, tag="w1_grouped", name="w1_grouped")
-
-        def interleave_w1(r, g, w1_grouped):
+        def interleave_w1(r, g):
+            w1_grouped = stage.tile([P, H1, PACK], BF16, align_bytes=64, tag="w1_grouped")
             v = W1_VECTOR_COLS
             interleave_rows(nc.vector.tensor_copy, w1_grouped[:, :v, :], w1_raw[:, r, g, :, :v])
             interleave_rows(nc.scalar.copy, w1_grouped[:, v:, :], w1_raw[:, r, g, :, v:])
@@ -168,17 +166,11 @@ def tile_infovae_pa_kernel(
                 banks.append(xt)
             return banks
 
-        def x_tile():
-            x_grouped = stage.tile([P, PASSES1 * PAIR_COLS * PACK], BF16, align_bytes=64, tag="x_grouped")
-            return x_grouped, x_grouped[:].bitcast(F32).rearrange("p (g b u) -> p g b u", g=PASSES1, u=2)
-
-        def by_column(bank):
-            return bank[:].rearrange("p u b -> p b u")
-
         def copy_x(banks):
-            x_grouped, words = x_tile()
+            x_grouped = stage.tile([P, PASSES1 * PAIR_COLS * PACK], BF16, align_bytes=64, tag="x_grouped")
+            words = x_grouped[:].bitcast(F32).rearrange("p (g b u) -> p g b u", g=PASSES1, u=2)
             for g in range(PASSES1):
-                nc.scalar.copy(out=words[:, g], in_=by_column(banks[g]))
+                nc.scalar.copy(out=words[:, g], in_=banks[g][:].rearrange("p u b -> p b u"))
             return x_grouped
 
         def quantise_x(j, x_grouped):
@@ -351,29 +343,22 @@ def tile_infovae_pa_kernel(
             for n in range(2):
                 nc.sync.dma_start(out=out_rows[n][:, row : row + tiles, :], in_=part[:, n])
 
-        def copy_x_and_interleave(xt):
-            x_grouped, words = x_tile()
-            grouped = w1_tile()
-            nc.scalar.copy(out=words[:, 0], in_=by_column(xt[0]))
-            interleave_w1(SIG, 1, grouped)
-            nc.vector.tensor_copy(out=words[:, 1], in_=by_column(xt[1]))
-            return x_grouped, grouped
-
         with tc.manual_schedule():
-            sig_grouped_0 = interleave_w1(SIG, 0, w1_tile())
+            sig_grouped_0 = interleave_w1(SIG, 0)
             xt = transpose_x(0)
             quantise_w1(SIG, 0, sig_grouped_0)
-            x_raw, sig_grouped_1 = copy_x_and_interleave(xt)
+            x_raw = copy_x(xt)
+            sig_grouped_1 = interleave_w1(SIG, 1)
             quantise_x(0, x_raw)
             quantise_w1(SIG, 1, sig_grouped_1)
             xt = transpose_x(1)
             transpose_biases()
             banks_sig = layer1(0, SIG)
             x_raw = copy_x(xt)
-            mu_grouped_0 = interleave_w1(MU, 0, w1_tile())
+            mu_grouped_0 = interleave_w1(MU, 0)
             quantise_x(1, x_raw)
             planes_sig = activate(SIG, banks_sig)
-            mu_grouped_1 = interleave_w1(MU, 1, w1_tile())
+            mu_grouped_1 = interleave_w1(MU, 1)
             quantise_w1(MU, 0, mu_grouped_0)
             banks_sig = layer1(1, SIG)
             xt = transpose_x(2)

@@ -29,6 +29,7 @@ H_TILES = H1 // P
 CHUNKS = PAIRS
 CHUNK_TILES = B_TILES // CHUNKS
 CHUNK_COLS = CHUNK_TILES * P
+PSUM_COLS = 512
 BIASES = 2 * H_TILES + 2
 W1_VECTOR_COLS = 320
 
@@ -62,8 +63,8 @@ def tile_infovae_pa_kernel(
 
         ident = keep.tile([P, P], F32)
         make_identity(nc, ident[:])
-        ident_cols = keep.tile([P, BIASES], BF16)
-        nc.gpsimd.tensor_copy(out=ident_cols[:], in_=ident[:, 0:BIASES])
+        ident_bf16 = keep.tile([P, P], BF16)
+        nc.gpsimd.tensor_copy(out=ident_bf16[:], in_=ident[:])
 
         bias_rows = keep.tile([P, P], BF16)
         nc.vector.memset(bias_rows[:], 0.0)
@@ -82,8 +83,8 @@ def tile_infovae_pa_kernel(
                 in_=w1[r][K_PASS * g : K_PASS * (g + 1), :].rearrange("(u p e) c -> p u (e c)", u=2, e=2),
             )
 
-        load_w1(SIG, 0)
         load_x_pair(0)
+        load_w1(SIG, 0)
         load_w1(SIG, 1)
         for r in (MU, SIG):
             nc.sync.dma_start(
@@ -107,7 +108,7 @@ def tile_infovae_pa_kernel(
 
         def transpose_biases():
             bias_ps = psum_o.tile([P, BIASES], F32, tag="out0")
-            nc.tensor.matmul(bias_ps[:], lhsT=bias_rows[:], rhs=ident_cols[:], start=True, stop=True)
+            nc.tensor.matmul(bias_ps[:], lhsT=bias_rows[:], rhs=ident_bf16[:, 0:BIASES], start=True, stop=True)
             nc.vector.tensor_copy(out=bias_col[:], in_=bias_ps[:])
             for e, slope in enumerate((1.0, NEG_SLOPE)):
                 nc.gpsimd.tensor_scalar(
@@ -343,13 +344,23 @@ def tile_infovae_pa_kernel(
             for n in range(2):
                 nc.sync.dma_start(out=out_rows[n][:, row : row + tiles, :], in_=part[:, n])
 
+        idle_rows = keep.tile([P, PSUM_COLS], BF16)
+        nc.vector.memset(idle_rows[:], 0.0)
+
+        def warm_up(products):
+            bank = psum_h.tile([P, PSUM_COLS], F32, tag="bank0", name="bank")
+            for n in range(products):
+                nc.tensor.matmul(bank[:], lhsT=ident_bf16[:], rhs=idle_rows[:], start=True, stop=True)
+
         with tc.manual_schedule():
-            sig_grouped_0 = interleave_w1(SIG, 0)
+            warm_up(4)
             xt = transpose_x(0)
-            quantise_w1(SIG, 0, sig_grouped_0)
+            warm_up(5)
             x_raw = copy_x(xt)
-            sig_grouped_1 = interleave_w1(SIG, 1)
+            sig_grouped_0 = interleave_w1(SIG, 0)
             quantise_x(0, x_raw)
+            sig_grouped_1 = interleave_w1(SIG, 1)
+            quantise_w1(SIG, 0, sig_grouped_0)
             quantise_w1(SIG, 1, sig_grouped_1)
             xt = transpose_x(1)
             transpose_biases()

import math
from contextlib import ExitStack

import concourse.mybir as mybir
from concourse.masks import make_identity

F32 = mybir.dt.float32
BF16 = mybir.dt.bfloat16
U32 = mybir.dt.uint32
U8 = mybir.dt.uint8
FP8X4 = mybir.dt.float8_e4m3fn_x4
ALU = mybir.AluOpType
ACT = mybir.ActivationFunctionType

P = 128
PACK = 4
K_PASS = P * PACK

B, H0, H1, H2 = 1024, 1024, 512, 128
NEG_SLOPE = 0.01
LV_MIN, LV_MAX = -10.0, 10.0
STD_MIN, STD_MAX = math.exp(0.5 * LV_MIN), math.exp(0.5 * LV_MAX)

B_TILES = B // P
PAIRS = B_TILES // 2
PAIR_COLS = 2 * P
PASSES1 = H0 // K_PASS
H_TILES = H1 // P
CHUNKS = PAIRS
CHUNK_TILES = B_TILES // CHUNKS
CHUNK_COLS = CHUNK_TILES * P
PSUM_COLS = 512
BIASES = 2 * H_TILES + 2
W1_VECTOR_COLS = 320

MU, SIG = 0, 1

FLOPS = 2 * (2 * B * H0 * H1 + 2 * B * H1 * H2)


def interleave_rows(copy, grouped, planes):
    copy(
        out=grouped.rearrange("p (c i) t -> p c t i", i=4),
        in_=planes.rearrange("p t (c i) -> p c t i", i=4),
    )


def tile_infovae_pa_kernel(
    tc, x, noise_enc, noise_z, w1_mu, b1_mu, w2_mu, b2_mu, w1_sig, b1_sig, w2_sig, b2_sig, out_0, out_1
):
    nc = tc.nc
    w1 = (w1_mu, w1_sig)
    w2 = (w2_mu, w2_sig)
    b1 = (b1_mu, b1_sig)
    b2 = (b2_mu, b2_sig)

    with ExitStack() as ctx:
        keep = ctx.enter_context(tc.tile_pool(name="keep", bufs=1))
        stage = ctx.enter_context(tc.tile_pool(name="stage", bufs=3))
        psum_t = ctx.enter_context(tc.psum_pool(name="psum_t", bufs=2))
        psum_h = ctx.enter_context(tc.psum_pool(name="psum_h", bufs=2))
        psum_o = ctx.enter_context(tc.psum_pool(name="psum_o", bufs=1))

        ident = keep.tile([P, P], F32)
        make_identity(nc, ident[:])
        ident_bf16 = keep.tile([P, P], BF16)
        nc.gpsimd.tensor_copy(out=ident_bf16[:], in_=ident[:])

        bias_rows = keep.tile([P, P], BF16)
        nc.vector.memset(bias_rows[:], 0.0)
        x_sb = keep.tile([P, B_TILES, H0], BF16)
        x_rows = x.rearrange("(p i) k -> p i k", i=B_TILES)
        w1_raw = keep.tile([P, 2, PASSES1, PACK, H1], BF16)
        w2_raw = keep.tile([P, 2, PACK, H2], BF16)
        noise = keep.tile([P, 2, B_TILES, H2], BF16)

        def load_x_pair(j):
            nc.sync.dma_start(out=x_sb[:, 2 * j : 2 * j + 2, :], in_=x_rows[:, 2 * j : 2 * j + 2, :])

        def load_w1(r, g):
            nc.sync.dma_start(
                out=w1_raw[:, r, g].rearrange("p (u e) c -> p u (e c)", e=2),
                in_=w1[r][K_PASS * g : K_PASS * (g + 1), :].rearrange("(u p e) c -> p u (e c)", u=2, e=2),
            )

        load_x_pair(0)
        load_w1(SIG, 0)
        load_w1(SIG, 1)
        for r in (MU, SIG):
            nc.sync.dma_start(
                out=bias_rows[H_TILES * r : H_TILES * (r + 1), :], in_=b1[r].rearrange("(m p) -> m p", p=P)
            )
            nc.sync.dma_start(
                out=bias_rows[2 * H_TILES + r : 2 * H_TILES + r + 1, :], in_=b2[r].rearrange("(a o) -> a o", a=1)
            )
        load_x_pair(1)
        load_w1(MU, 0)
        load_w1(MU, 1)
        for r in (SIG, MU):
            nc.sync.dma_start(out=w2_raw[:, r], in_=w2[r].rearrange("(m p) o -> p m o", p=P))
        load_x_pair(2)
        load_x_pair(3)
        nc.sync.dma_start(out=noise[:, 0], in_=noise_enc.rearrange("(p i) o -> p i o", i=B_TILES))
        nc.sync.dma_start(out=noise[:, 1], in_=noise_z.rearrange("(p i) o -> p i o", i=B_TILES))

        bias_col = keep.tile([P, BIASES], F32)
        half_b2_sig = keep.tile([P, 2], F32)

        def transpose_biases():
            bias_ps = psum_o.tile([P, BIASES], F32, tag="out0")
            nc.tensor.matmul(bias_ps[:], lhsT=bias_rows[:], rhs=ident_bf16[:, 0:BIASES], start=True, stop=True)
            nc.vector.tensor_copy(out=bias_col[:], in_=bias_ps[:])
            for e, slope in enumerate((1.0, NEG_SLOPE)):
                nc.gpsimd.tensor_scalar(
                    out=half_b2_sig[:, e : e + 1],
                    in0=bias_col[:, BIASES - 1 : BIASES],
                    scalar1=0.5 * slope,
                    scalar2=0.0,
                    op0=ALU.mult,
                    op1=ALU.add,
                )

        w2_grouped = keep.tile([P, 2, H2, PACK], BF16, align_bytes=64)
        w2_codes = keep.tile([P, 2 * H2], U32, align_bytes=64)
        w2_scales = keep.tile([P, 2 * H2], U8, align_bytes=64)

        def interleave_w2(r):
            nc.vector.tensor_copy(out=w2_grouped[:, r], in_=w2_raw[:, r].rearrange("p m o -> p o m"))

        def quantise_w2():
            nc.vector.quantize_mx(
                out=w2_codes[:].bitcast(FP8X4),
                scales=w2_scales[:],
                in_=w2_grouped[:].rearrange("p r o m -> p (r o m)"),
            )

        x_codes = keep.tile([P, PAIRS, PASSES1, PAIR_COLS], U32, align_bytes=64)
        x_scales = keep.tile([P, PAIRS, PASSES1, PAIR_COLS], U8, align_bytes=64)
        w1_codes = keep.tile([P, 2, PASSES1, H1], U32, align_bytes=64)
        w1_scales = keep.tile([P, 2, PASSES1, H1], U8, align_bytes=64)

        def interleave_w1(r, g):
            w1_grouped = stage.tile([P, H1, PACK], BF16, align_bytes=64, tag="w1_grouped")
            v = W1_VECTOR_COLS
            interleave_rows(nc.vector.tensor_copy, w1_grouped[:, :v, :], w1_raw[:, r, g, :, :v])
            interleave_rows(nc.scalar.copy, w1_grouped[:, v:, :], w1_raw[:, r, g, :, v:])
            return w1_grouped

        def quantise_w1(r, g, w1_grouped):
            nc.vector.quantize_mx(
                out=w1_codes[:, r, g, :].bitcast(FP8X4),
                scales=w1_scales[:, r, g, :],
                in_=w1_grouped[:].rearrange("p c t -> p (c t)"),
            )

        def transpose_x(j):
            banks = []
            for g in range(PASSES1):
                xt = psum_t.tile([P, 2, PAIR_COLS], F32, tag="xt")
                for ii in range(2):
                    words = x_sb[:, 2 * j + ii, :].bitcast(F32)
                    for u in range(2):
                        first = (K_PASS * g + 2 * P * u) // 2
                        nc.tensor.transpose(
                            xt[:, u, P * ii : P * (ii + 1)], words[:, first : first + P], ident[:]
                        )
                banks.append(xt)
            return banks

        def copy_x(banks):
            x_grouped = stage.tile([P, PASSES1 * PAIR_COLS * PACK], BF16, align_bytes=64, tag="x_grouped")
            words = x_grouped[:].bitcast(F32).rearrange("p (g b u) -> p g b u", g=PASSES1, u=2)
            for g in range(PASSES1):
                nc.scalar.copy(out=words[:, g], in_=banks[g][:].rearrange("p u b -> p b u"))
            return x_grouped

        def quantise_x(j, x_grouped):
            nc.vector.quantize_mx(
                out=x_codes[:, j].rearrange("p g b -> p (g b)").bitcast(FP8X4),
                scales=x_scales[:, j].rearrange("p g b -> p (g b)"),
                in_=x_grouped[:],
            )

        def layer1(c, r):
            banks = []
            for m in range(H_TILES):
                units = slice(P * m, P * (m + 1))
                if m % 2 == 0:
                    banks.append(psum_h.tile([P, 2, CHUNK_COLS], F32, tag="bank%d" % r, name="bank"))
                for g in range(PASSES1):
                    nc.tensor.matmul_mx(
                        out=banks[m // 2][:, m % 2, :],
                        lhsT=w1_codes[:, r, g, units].bitcast(FP8X4),
                        lhsT_scale=w1_scales[:, r, g, units],
                        rhs=x_codes[:, c, g, :].bitcast(FP8X4),
                        rhs_scale=x_scales[:, c, g, :],
                        start=(g == 0),
                        stop=(g == PASSES1 - 1),
                    )
            return banks

        def activate(r, banks):
            planes = stage.tile([P, H_TILES, CHUNK_COLS], BF16 if r == SIG else F32, tag="planes%d" % r)
            for m in range(H_TILES):
                nc.scalar.activation(
                    out=planes[:, m, :],
                    in_=banks[m // 2][:, m % 2, :],
                    func=ACT.Tanh if r == SIG else ACT.Identity,
                    bias=bias_col[:, H_TILES * r + m : H_TILES * r + m + 1],
                    scale=1.0,
                )
            return planes

        def interleave_sig(copy, planes):
            h_grouped = stage.tile([P, CHUNK_COLS, PACK], BF16, align_bytes=64, tag="h_grouped1")
            interleave_rows(copy, h_grouped[:], planes[:])
            return h_grouped

        def lrelu_mu(planes, n=CHUNK_COLS, first=0):
            h_grouped = stage.tile([P, n, PACK], BF16, align_bytes=64, tag="h_grouped0")
            columns = planes[:, :, first : first + n].rearrange("p m b -> p b m")
            nc.vector.scalar_tensor_tensor(
                out=h_grouped[:], in0=columns, scalar=NEG_SLOPE, in1=columns, op0=ALU.mult, op1=ALU.max
            )
            return h_grouped

        def quantise_h(r, h_grouped, n):
            h_codes = stage.tile([P, n], U32, align_bytes=64, tag="h_codes%d" % r)
            h_scales = stage.tile([P, n], U8, align_bytes=64, tag="h_scales%d" % r)
            nc.vector.quantize_mx(
                out=h_codes[:].bitcast(FP8X4), scales=h_scales[:], in_=h_grouped[:].rearrange("p b m -> p (b m)")
            )
            return h_codes, h_scales

        def layer2(r, h_grouped):
            h_codes, h_scales = quantise_h(r, h_grouped, CHUNK_COLS)
            outs = slice(H2 * r, H2 * (r + 1))
            acc = psum_o.tile([P, CHUNK_COLS], F32, tag="out%d" % r)
            nc.tensor.matmul_mx(
                out=acc[:],
                lhsT=w2_codes[:, outs].bitcast(FP8X4),
                lhsT_scale=w2_scales[:, outs],
                rhs=h_codes[:].bitcast(FP8X4),
                rhs_scale=h_scales[:],
                start=True,
                stop=True,
            )
            return acc

        def layer2_mu_rows(h_grouped, bank):
            h_codes, h_scales = quantise_h(MU, h_grouped, P)
            acc = psum_o.tile([P, H2], F32, tag="out%d" % bank)
            nc.tensor.matmul_mx(
                out=acc[:],
                lhsT=h_codes[:].bitcast(FP8X4),
                lhsT_scale=h_scales[:],
                rhs=w2_codes[:, 0:H2].bitcast(FP8X4),
                rhs_scale=w2_scales[:, 0:H2],
                start=True,
                stop=True,
            )
            return acc

        b2_mu_rows = keep.tile([P, H2], F32)

        def spread_b2_mu():
            spread = psum_t.tile([P, H2], F32, tag="xt", name="spread")
            nc.tensor.matmul(
                spread[:],
                lhsT=bias_col[:, BIASES - 2 : BIASES - 1].to_broadcast([P, P]),
                rhs=ident[:],
                start=True,
                stop=True,
            )
            nc.scalar.copy(out=b2_mu_rows[:], in_=spread[:])

        def exponentials(acc):
            exps = stage.tile([P, 2, CHUNK_COLS], F32, tag="exps")
            for e, slope in enumerate((1.0, NEG_SLOPE)):
                nc.scalar.activation(
                    out=exps[:, e, :], in_=acc[:], func=ACT.Exp, bias=half_b2_sig[:, e : e + 1], scale=0.5 * slope
                )
            return exps

        def transpose_back(rows):
            turned = psum_t.tile([P, CHUNK_TILES, H2], F32, tag="xt", name="turned")
            for i in range(CHUNK_TILES):
                nc.tensor.transpose(turned[:, i, :], rows[:, P * i : P * (i + 1)], ident[:])
            return turned

        def std_of(exps):
            std = stage.tile([P, CHUNK_COLS], F32, tag="std")
            nc.vector.scalar_tensor_tensor(
                out=std[:], in0=exps[:, 0, :], scalar=STD_MIN, in1=exps[:, 1, :], op0=ALU.max, op1=ALU.max
            )
            return transpose_back(std)

        def biased_mean(acc):
            biased = stage.tile([P, CHUNK_COLS], F32, tag="biased")
            nc.scalar.activation(
                out=biased[:], in_=acc[:], func=ACT.Identity, bias=bias_col[:, BIASES - 2 : BIASES - 1], scale=1.0
            )
            return biased

        def lrelu_mean(biased, n):
            mean = stage.tile([P, n], F32, tag="mean")
            nc.vector.scalar_tensor_tensor(
                out=mean[:], in0=biased[:], scalar=NEG_SLOPE, in1=biased[:], op0=ALU.mult, op1=ALU.max
            )
            return mean

        def mean_of(biased):
            return transpose_back(lrelu_mean(biased, CHUNK_COLS))

        def biased_rows(acc):
            biased = stage.tile([P, H2], F32, tag="biased")
            nc.vector.tensor_tensor(out=biased[:], in0=acc[:], in1=b2_mu_rows[:], op=ALU.add)
            return biased

        out_rows = (
            out_0.rearrange("(p i) o -> p i o", i=B_TILES),
            out_1.rearrange("(p i) o -> p i o", i=B_TILES),
        )
        both = [P, 2, CHUNK_TILES, H2]

        def scale_noise(c, std):
            z = stage.tile(both, F32, tag="z")
            nc.vector.scalar_tensor_tensor(
                out=z[:],
                in0=std[:].unsqueeze(1).to_broadcast(both),
                scalar=STD_MAX,
                in1=noise[:, :, CHUNK_TILES * c : CHUNK_TILES * (c + 1), :],
                op0=ALU.min,
                op1=ALU.mult,
            )
            return z

        def add_mean(c, z, mean, first=0, tiles=CHUNK_TILES):
            part = z[:, :, first : first + tiles, :]
            nc.vector.tensor_tensor(
                out=part, in0=part, in1=mean.unsqueeze(1).to_broadcast([P, 2, tiles, H2]), op=ALU.add
            )
            row = CHUNK_TILES * c + first
            for n in range(2):
                nc.sync.dma_start(out=out_rows[n][:, row : row + tiles, :], in_=part[:, n])

        idle_rows = keep.tile([P, PSUM_COLS], BF16)
        nc.vector.memset(idle_rows[:], 0.0)

        def warm_up(products):
            bank = psum_h.tile([P, PSUM_COLS], F32, tag="bank0", name="bank")
            for n in range(products):
                nc.tensor.matmul(bank[:], lhsT=ident_bf16[:], rhs=idle_rows[:], start=True, stop=True)

        with tc.manual_schedule():
            warm_up(4)
            xt = transpose_x(0)
            warm_up(5)
            x_raw = copy_x(xt)
            sig_grouped_0 = interleave_w1(SIG, 0)
            quantise_x(0, x_raw)
            sig_grouped_1 = interleave_w1(SIG, 1)
            quantise_w1(SIG, 0, sig_grouped_0)
            quantise_w1(SIG, 1, sig_grouped_1)
            xt = transpose_x(1)
            transpose_biases()
            banks_sig = layer1(0, SIG)
            x_raw = copy_x(xt)
            mu_grouped_0 = interleave_w1(MU, 0)
            quantise_x(1, x_raw)
            planes_sig = activate(SIG, banks_sig)
            mu_grouped_1 = interleave_w1(MU, 1)
            quantise_w1(MU, 0, mu_grouped_0)
            banks_sig = layer1(1, SIG)
            xt = transpose_x(2)
            interleave_w2(SIG)
            interleave_w2(MU)
            quantise_w1(MU, 1, mu_grouped_1)
            h_sig = interleave_sig(nc.vector.tensor_copy, planes_sig)
            quantise_w2()
            banks_mu = layer1(0, MU)
            acc_sig = layer2(SIG, h_sig)
        x_raw = copy_x(xt)
        spread_b2_mu()

        for c in range(CHUNKS):
            planes_mu = activate(MU, banks_mu)
            if c + 1 == CHUNKS:
                break
            banks_mu = layer1(c + 1, MU)
            if c == 0:
                quantise_x(2, x_raw)
                xt = transpose_x(3)
            planes_sig = activate(SIG, banks_sig)
            exps = exponentials(acc_sig)
            h_mu = lrelu_mu(planes_mu)
            if c > 0:
                add_mean(c - 1, z, mean[:])
            acc_mu = layer2(MU, h_mu)
            std = std_of(exps)
            if c + 2 < CHUNKS:
                banks_sig = layer1(c + 2, SIG)
            if c == 0:
                x_raw = copy_x(xt)
            if c + 2 < CHUNKS:
                h_sig = interleave_sig(nc.vector.tensor_copy, planes_sig)
            if c == 0:
                quantise_x(3, x_raw)
            biased = biased_mean(acc_mu)
            if c + 2 < CHUNKS:
                acc_sig = layer2(SIG, h_sig)
            z = scale_noise(c, std)
            mean = mean_of(biased)

        h_sig = interleave_sig(nc.scalar.copy, planes_sig)
        tiles = range(CHUNK_TILES)
        acc_sig = layer2(SIG, h_sig)
        h_mu = [lrelu_mu(planes_mu, P, 0)]
        exps = exponentials(acc_sig)
        acc_mu = [layer2_mu_rows(h_mu[0], MU)]
        std = std_of(exps)
        h_mu.append(lrelu_mu(planes_mu, P, P))
        add_mean(CHUNKS - 2, z, mean[:])
        acc_mu.append(layer2_mu_rows(h_mu[1], SIG))
        z = scale_noise(CHUNKS - 1, std)
        biased = [biased_rows(acc_mu[i]) for i in tiles]
        mean = [lrelu_mean(biased[i], P) for i in tiles]
        for i in tiles:
            add_mean(CHUNKS - 1, z, mean[i][:].unsqueeze(1), i, 1)
